import numpy as np
import ml_dtypes


def mxq(x, axis, fmt="e4m3"):
    dtype, down = {"e4m3": (ml_dtypes.float8_e4m3fn, 7), "e5m2": (ml_dtypes.float8_e5m2, 14)}[fmt]
    v = np.moveaxis(np.asarray(x, np.float32).astype(ml_dtypes.bfloat16).astype(np.float64), axis, -1)
    blocks = v.reshape(v.shape[:-1] + (-1, 32))
    amax = np.abs(blocks).max(-1, keepdims=True)
    byte = np.maximum(np.where(amax > 0, np.frexp(amax)[1] - 1 + 127, 0) - down, 1)
    scale = np.exp2(byte - 127.0)
    codes = (blocks / scale).astype(np.float32).astype(dtype).astype(np.float64)
    return np.moveaxis((codes * scale).reshape(v.shape), -1, axis)


WIDE = False


def mx_kscale(k):
    if not WIDE:
        return np.ones(k)
    levels = np.array([18, -18])
    if k % 512:
        return np.exp2(np.random.permutation(np.resize(levels, k // 32))).repeat(32)
    a = np.empty((k // 512, 16))
    for p in range(k // 512):
        a[p, :8] = np.random.permutation(np.resize(levels, 8))
        for g in range(8):
            far = levels[np.abs(levels - a[p, g]) >= 10]
            a[p, g + 8] = far[np.random.randint(len(far))]
    return np.exp2(a.ravel()).repeat(32)


BF16 = ml_dtypes.bfloat16


def bf(x):
    return np.asarray(x, np.float32).astype(BF16)


def f64(x):
    return np.asarray(x).astype(np.float64)


B, Hh, Ww, NB, BS, ORI, RI = 4, 4, 4, 2, 512, 8, 2
C = NB * BS
R = B * ORI * Hh * Ww


def split(a):
    return f64(a).transpose(5, 0, 2, 3, 4, 1).reshape(RI, R, NB, BS).transpose(0, 2, 1, 3)


def merge(a):
    return a.transpose(2, 1, 3, 0).reshape(B, ORI, Hh, Ww, C, RI).transpose(0, 4, 1, 2, 3, 5)


def setup_inputs():
    s = mx_kscale(R).reshape(B, 1, ORI, Hh, Ww, 1)
    u = mx_kscale(C)
    v = mx_kscale(C).reshape(NB, BS)
    ub = u.reshape(NB, BS)
    xh0 = bf(np.random.standard_normal((B, C, ORI, Hh, Ww, RI)))
    w1_0 = bf(np.random.standard_normal((RI, NB, BS, BS)) / np.sqrt(RI * BS))
    w2_0 = bf(np.random.standard_normal((RI, NB, BS, BS)) / np.sqrt(BS))
    b1 = bf(np.random.standard_normal((RI, NB, BS)) * 0.3)
    b2 = bf(np.random.standard_normal((RI, NB, BS)) * 0.3)
    g = np.random.standard_normal((B, C, ORI, Hh, Ww, RI)) * np.exp2(np.random.randint(-6, 1, (B, 1, ORI, Hh, Ww, 1)))
    x = split(xh0)
    w = f64(w1_0)
    b = f64(b1)[:, :, None, :]
    z1 = np.stack([x[0] @ w[0] - x[1] @ w[1] + b[0], x[0] @ w[1] + x[1] @ w[0] + b[1]])
    return {
        "xh": bf(f64(xh0) * s),
        "w1": bf(f64(w1_0) / v[None, :, None, :]),
        "w2": bf(f64(w2_0) * v[None, :, :, None] / ub[None, :, None, :]),
        "b1": b1,
        "b2": b2,
        "z1": np.asarray(z1, np.float32),
        "grad_out": bf(g / s * u[None, :, None, None, None, None]),
    }


def reference(xh, w1, w2, b1, b2, z1, grad_out):
    gq = mxq(split(grad_out), 3, "e5m2")
    w2t = mxq(f64(w2), 3, "e4m3").transpose(0, 1, 3, 2)
    dr = (gq[0] @ w2t[0]) + (gq[1] @ w2t[1])
    di = (gq[1] @ w2t[0]) - (gq[0] @ w2t[1])
    dz1 = np.where(f64(z1) > 0.0, np.stack([dr, di]), 0.0)
    dzh = mxq(dz1, 3, "e5m2")
    w1t = mxq(f64(w1), 3, "e4m3").transpose(0, 1, 3, 2)
    dxr = (dzh[0] @ w1t[0]) + (dzh[1] @ w1t[1])
    dxi = (dzh[1] @ w1t[0]) - (dzh[0] @ w1t[1])
    dzp = mxq(dz1, 2, "e5m2")
    xt = mxq(split(xh), 2, "e4m3").transpose(0, 1, 3, 2)
    dwr = (xt[0] @ dzp[0]) + (xt[1] @ dzp[1])
    dwi = (xt[0] @ dzp[1]) - (xt[1] @ dzp[0])
    return merge(np.stack([dxr, dxi])), np.stack([dwr, dwi])

@@ -1,0 +1,332 @@
+from contextlib import ExitStack
+
+import concourse.mybir as mybir
+from concourse.masks import make_identity
+
+F32 = mybir.dt.float32
+BF16 = mybir.dt.bfloat16
+U32 = mybir.dt.uint32
+U8 = mybir.dt.uint8
+E4 = mybir.dt.float8_e4m3fn_x4
+E5 = mybir.dt.float8_e5m2_x4
+ALU = mybir.AluOpType
+
+P = 128
+NB = 2
+BS = 512
+FLOPS = 12 * NB * 2 * BS * BS * BS
+BYTES = 4 * (2 * 1024 * 1024) + 4 * 1024 * 1024 + 8 * 1024 * 1024
+
+ORDER = """
+Lg:2:0:D Lg:0:0:D GC:20:0:V Lw2:1:0:D GC:00:0:V WT:210:0:P Lw2:0:0:D WT:211:0:P
+GC:30:0:V GC:10:0:V GN:-:0:V GC:21:0:V GQ:0:0:V WT:200:0:P GC:01:0:S WC:210:0:S
+WC:211:0:S WC:200:0:S GC:31:0:V WT:201:0:P WC:201:0:S Lw1:0:0:D WT:100:0:P WC:100:0:S
+Lw1:1:0:D WT:101:0:P GC:11:0:V Lz:0:0:D WT:111:0:P WC:101:0:S WQ:21:0:V WQ:20:0:V
+WT:110:0:P WC:110:0:S WC:111:0:S GQ:1:0:V S1:03:0:P GNQ:-:0:V Lg:0:1:D S1:00:0:P
+WQ:10:0:V S1:02:0:P ST:03:0:V GC:01:1:S GC:00:1:S ST:00:0:V S1:01:0:P Lg:2:1:D
+GC:30:1:S Lw2:1:1:D GC:11:1:V GC:21:1:S S1:10:0:P S1:11:0:P ST:01:0:V ST:02:0:V
+Lw2:0:1:D Lw1:1:1:D S1:12:0:P S1:13:0:P WT:210:1:P GC:31:1:V Lz:1:0:D WC:210:1:S
+GC:10:1:V WT:211:1:P WT:201:1:P WC:211:1:S WT:200:1:P GC:20:1:V WT:110:1:P WQ:11:0:V
+WC:201:1:S GN:-:1:V DI:01:0:V Lx:0:0:D WQ:21:1:V WT:111:1:P DT:01:0:P Lx:1:0:D
+GQ:1:1:V DT:00:0:P WC:200:1:S WQ:20:1:V GQ:0:1:V WC:110:1:S WC:111:1:S S1:00:1:P
+S1:03:1:P DC:00:0:S S1:01:1:P S1:02:1:P ST:10:0:V ST:11:0:V ST:12:0:V Lx:2:0:D
+DC:01:0:S Lx:3:0:D DI:00:0:S DT:10:0:P DC:10:0:S ST:13:0:V DN:-:0:V DT:11:0:P
+Lz:0:1:D DC:11:0:S XT:1:0:P GNQ:-:1:V Lz:1:1:D S1:13:1:P XC:1:0:S XT:0:0:P
+DI:10:0:S XT:3:0:P XT:2:0:P DPQ:0:0:V DI:11:0:V S1:11:1:P XC:3:0:S XC:0:0:S
+DKQ:1:0:V O0:13:0:P ST:00:1:V Lw1:0:1:D O0:10:0:P O0:11:0:P ST:03:1:V S1:12:1:P
+XC:2:0:S ST:01:1:V ST:02:1:V DT:01:1:P WT:100:1:P Lx:2:1:D ST:13:1:V ST:11:1:V
+DKQ:0:0:V DT:00:1:P ST:12:1:V E0:13:0:S O0:12:0:P E0:10:0:S WC:100:1:S E0:11:0:S
+S1:10:1:P XQ:0:0:V O0:03:0:P XN:-:0:V XQ:1:0:V Lx:3:1:D DPQ:1:0:V E0:12:0:S
+O0:00:0:P O0:01:0:P Lx:0:1:D Lx:1:1:D DC:01:1:V F0:12:0:D ST:10:1:V DC:00:1:S
+O0:02:0:P E0:03:0:S E0:00:0:S DT:11:1:P DC:11:1:S DN:-:1:V XNQ:-:0:V XT:3:1:P
+F0:10:0:D WT:101:1:P E0:02:0:S DT:10:1:P O1:13:0:P DI:10:1:V DI:01:1:V DI:00:1:V
+F0:02:0:D WQ:11:1:V WC:101:1:S WQ:10:1:V O1:12:0:P E0:01:0:S DC:10:1:V O1:01:0:P
+E1:13:0:S O1:00:0:P O1:11:0:P XC:3:1:S E1:12:0:S O1:02:0:P E1:01:0:S DI:11:1:V
+DKQ:1:1:V O1:03:0:P O1:10:0:P DKQ:0:1:V E1:11:0:V E1:02:0:S E1:10:0:V XT:2:1:P
+E1:03:0:S F0:00:0:D XT:1:1:P XC:1:1:V F1:12:0:D F1:02:0:D E1:00:0:S XC:2:1:S
+XT:0:1:P O0:02:1:P E0:02:1:V DPQ:1:1:V XC:0:1:S O0:03:1:P XQ:1:1:V E0:03:1:S
+O0:11:1:P O0:10:1:P E0:11:1:S F1:00:0:D F1:10:0:D DPQ:0:1:V E0:10:1:S O0:13:1:P
+E0:13:1:S O0:12:1:P F0:02:1:D E0:12:1:S O0:01:1:P F0:10:1:D O0:00:1:P F0:12:1:D
+XQ:0:1:V O1:00:1:P XN:-:1:V XNQ:-:1:V E0:01:1:S E0:00:1:S F0:00:1:D O1:01:1:P
+O1:11:1:P E1:00:1:V E1:01:1:S F1:00:1:D O1:10:1:P O1:03:1:P E1:11:1:V O1:02:1:P
+E1:02:1:V E1:10:1:S F1:10:1:D O1:12:1:P E1:12:1:V O1:13:1:P E1:03:1:S F1:02:1:D
+E1:13:1:S F1:12:1:D
+"""
+T_BANKS = 3
+M_BANKS = 5
+OUT_BUFS = 10
+
+
+def tile_scatteringmodule_pa_v_kernel(tc, xh, w1, w2, b1, b2, z1, grad_out, out_0, out_1):
+    nc = tc.nc
+    g_hbm = grad_out.rearrange("b (n p t) o h w r -> n p b (t o h w r)", n=NB, t=4)
+    x_hbm = xh.rearrange("b (n p t) o h w r -> n p b (t o h w r)", n=NB, t=4)
+    w_hbm = {"1": w1.rearrange("r n (p a) k -> r n p a k", a=4), "2": w2.rearrange("r n (p a) k -> r n p a k", a=4)}
+    z_hbm = z1.rearrange("r n (m t) k -> r n m t k", t=4)
+    o0_hbm = out_0.rearrange("b (n p a) o h w r -> n p b (a o h w r)", n=NB, a=4)
+    o1_hbm = out_1.rearrange("r n (p a) k -> r n p a k", a=4)
+
+    with ExitStack() as ctx:
+        const = ctx.enter_context(tc.tile_pool(name="const", bufs=1))
+        raw = ctx.enter_context(tc.tile_pool(name="raw", bufs=1))
+        grp = ctx.enter_context(tc.tile_pool(name="grp", bufs=1))
+        mx = ctx.enter_context(tc.tile_pool(name="mx", bufs=1))
+        outs = ctx.enter_context(tc.tile_pool(name="outs", bufs=OUT_BUFS))
+        tps = ctx.enter_context(tc.psum_pool(name="tps", bufs=T_BANKS))
+        mps = ctx.enter_context(tc.psum_pool(name="mps", bufs=M_BANKS))
+
+        ident = const.tile([P, P], F32, name="ident")
+        make_identity(nc, ident[:])
+
+        def quant(cs, grouped, lo, hi, fmt):
+            nc.vector.quantize_mx(
+                out=cs[0][:, lo:hi].bitcast(fmt), scales=cs[1][:, lo:hi], in_=grouped[:, 4 * lo : 4 * hi]
+            )
+
+        def mm(out, l, llo, lf, r, rlo, rf, start, stop):
+            nc.tensor.matmul_mx(
+                out=out,
+                lhsT=l[0][:, llo : llo + 128].bitcast(lf),
+                lhsT_scale=l[1][:, llo : llo + 128],
+                rhs=r[0][:, rlo : rlo + 512].bitcast(rf),
+                rhs_scale=r[1][:, rlo : rlo + 512],
+                start=start,
+                stop=stop,
+            )
+
+        tiles = {}
+
+        def get(n, key, shape, dt, pool, bufs=1):
+            if (n, key) not in tiles:
+                t = pool.tile(shape, dt, name=key, tag=key, bufs=bufs, align_bytes=64)
+                tiles[n, key] = t
+            return tiles[n, key]
+
+        def codes(n, key, width, bufs=1):
+            return get(n, key + "_c", [P, width], U32, mx, bufs), get(n, key + "_s", [P, width], U8, mx, bufs)
+
+        def bank(n, key, shape, pool, tag):
+            t = pool.tile(shape, F32, name=tag, tag=tag)
+            tiles[n, key] = t
+            return t
+
+        def copy(engine):
+            return nc.vector.tensor_copy if engine == "V" else nc.scalar.copy
+
+        def g_raw(n):
+            return get(n, "g_raw", [P, 4, 4, 256], BF16, raw)
+
+        def x_raw(n):
+            return get(n, "x_raw", [P, 4, 4, 256], BF16, raw)
+
+        def w_raw(n, k, r):
+            return get(n, "w%s_raw%d" % (k, r), [P, 4, BS], BF16, raw)
+
+        def z_raw(n, r):
+            return get(n, "z_raw%d" % r, [P, 4, BS], F32, raw)
+
+        def g_grp(n):
+            return get(n, "g_grp", [P, 3, 4, P, 4], BF16, grp)
+
+        def w_grp(n, k):
+            return get(n, "w%s_grp" % k, [P, 2, 4, P, 4], BF16, grp)
+
+        def dz_tile(n, r):
+            return get(n, "dz%d" % r, [P, 4, BS], BF16, grp)
+
+        def dp_grp(n):
+            return get(n, "dp_grp", [P, 2, BS, 4], BF16, grp)
+
+        def dk_grp(n):
+            return get(n, "dk_grp", [P, 2, 3, 256, 4], BF16, grp)
+
+        def x_grp(n):
+            return get(n, "x_grp", [P, 3, 4, P, 4], BF16, grp)
+
+        def out_tile(n, key, shape):
+            if (n, key) not in tiles:
+                t = outs.tile(shape, F32, name="o", tag="o")
+                tiles[n, key] = t
+            return tiles[n, key]
+
+        def Lg(n, b, j, e):
+            nc.sync.dma_start(
+                out=g_raw(n)[:, b : b + 2].rearrange("p b t q -> p b (t q)"), in_=g_hbm[n][:, b : b + 2, :]
+            )
+
+        def Lx(n, b, j, e):
+            nc.sync.dma_start(out=x_raw(n)[:, :, b, :], in_=x_hbm[n][:, b, :].rearrange("p (a q) -> p a q", a=4))
+
+        def Lw1(n, r, j, e):
+            nc.sync.dma_start(out=w_raw(n, "1", r)[:], in_=w_hbm["1"][r][n])
+
+        def Lw2(n, r, j, e):
+            nc.sync.dma_start(out=w_raw(n, "2", r)[:], in_=w_hbm["2"][r][n])
+
+        def Lz(n, r, j, e):
+            nc.sync.dma_start(out=z_raw(n, r)[:], in_=z_hbm[r][n])
+
+        def GC(n, b, ri, e):
+            src = g_raw(n)[:, b].rearrange("p t (m j r) -> p r m j t", j=4, r=2)[:, ri]
+            dst = g_grp(n)[:, ri, :, 32 * b : 32 * b + 32, :].rearrange("p j m t -> p m j t")
+            copy(e)(out=dst, in_=src)
+
+        def GQ(n, ri, j, e):
+            quant(codes(n, "g", 1536), g_grp(n)[:].rearrange("p s j m t -> p (s j m t)"), 512 * ri, 512 * ri + 512, E5)
+
+        def GN(n, i, j, e):
+            gg = g_grp(n)[:].rearrange("p s j m t -> p s (j m t)")
+            nc.vector.tensor_scalar_mul(out=gg[:, 2], in0=gg[:, 0], scalar1=-1.0)
+
+        def GNQ(n, i, j, e):
+            quant(codes(n, "g", 1536), g_grp(n)[:].rearrange("p s j m t -> p (s j m t)"), 1024, 1536, E5)
+
+        def WT(n, k, r, half):
+            words = w_raw(n, k, r)[:].rearrange("p a k -> p (a k)").bitcast(F32)
+            t = bank(n, "wt%s%d%d" % (k, r, half), [P, 2, 2, P], tps, "tp")
+            for a in range(2):
+                for u in range(2):
+                    lo = (2 * half + a) * 256 + u
+                    nc.tensor.transpose(t[:, a, u, :], words[:, lo : lo + 255 : 2], ident[:])
+
+        def WC(n, k, r, half, e):
+            t = tiles[n, "wt%s%d%d" % (k, r, half)]
+            dst = w_grp(n, k)[:, r, 2 * half : 2 * half + 2].rearrange("p a m t -> p (a m t)").bitcast(F32)
+            copy(e)(out=dst.rearrange("p (a m u) -> p a m u", a=2, u=2), in_=t[:].rearrange("p a u m -> p a m u"))
+
+        def WQ(n, k, r):
+            quant(
+                codes(n, "w" + k, 1024, 2 if k == "1" else 1),
+                w_grp(n, k)[:].rearrange("p r a m t -> p (r a m t)"),
+                512 * r,
+                512 * r + 512,
+                E4,
+            )
+
+        def S1(n, r, j, e):
+            t = bank(n, "s1%d%d" % (r, j), [P, BS], mps, "mm")
+            gc, wc = codes(n, "g", 1536), codes(n, "w2", 1024)
+            pairs = ((0, 0), (512, 512)) if r == 0 else ((512, 0), (1024, 512))
+            for i, (glo, wlo) in enumerate(pairs):
+                mm(t[:], gc, glo + 128 * j, E5, wc, wlo, E4, i == 0, i == 1)
+
+        def ST(n, r, j, e):
+            t = tiles[n, "s1%d%d" % (r, j)]
+            z = z_raw(n, r)[:, j].rearrange("p (k u e) -> p u k e", u=2, e=2)
+            dz = dz_tile(n, r)[:, j].rearrange("p (u k e) -> p u k e", u=2, e=2)
+            b4 = t[:].rearrange("p (u e k) -> p u k e", u=2, e=2)
+            for u in range(2):
+                nc.vector.scalar_tensor_tensor(
+                    out=dz[:, u], in0=z[:, u], scalar=0.0, in1=b4[:, u], op0=ALU.is_gt, op1=ALU.mult
+                )
+
+        def DI(n, r, hf, e):
+            k = slice(256 * hf, 256 * hf + 256)
+            copy(e)(out=dp_grp(n)[:, r, k, :], in_=dz_tile(n, r)[:, :, k].rearrange("p t k -> p k t"))
+
+        def DPQ(n, r, j, e):
+            quant(codes(n, "dp", 1024, 2), dp_grp(n)[:].rearrange("p r k t -> p (r k t)"), 512 * r, 512 * r + 512, E5)
+
+        def DT(n, r, u, e):
+            words = dz_tile(n, r)[:].rearrange("p t k -> p (t k)").bitcast(F32)
+            t = bank(n, "dt%d%d" % (r, u), [P, 2, 2, P], tps, "tp")
+            for i in range(2):
+                for v in range(2):
+                    lo = (2 * u + i) * 256 + v * 128
+                    nc.tensor.transpose(t[:, i, v, :], words[:, lo : lo + 128], ident[:])
+
+        def DC(n, r, u, e):
+            t = tiles[n, "dt%d%d" % (r, u)]
+            dst = dk_grp(n)[:].rearrange("p h s q t -> p (h s q t)").bitcast(F32)
+            dst = dst.rearrange("p (h s m x) -> p s h m x", h=2, s=3, x=8)[:, r]
+            dst = dst[:, :, :, 4 * u : 4 * u + 4].rearrange("p h m (e v) -> p h m e v", e=2)
+            copy(e)(out=dst, in_=t[:].rearrange("p e v (h m) -> p h m e v", h=2))
+
+        def DN(n, i, j, e):
+            d = dk_grp(n)[:].rearrange("p h s q t -> p s h (q t)")
+            nc.vector.tensor_scalar_mul(out=d[:, 2], in0=d[:, 0], scalar1=-1.0)
+
+        def DKQ(n, h, j, e):
+            d = dk_grp(n)[:].rearrange("p h s q t -> p (h s q t)")
+            cs = codes(n, "dk", 1536, 2)
+            quant(cs, d, 768 * h, 768 * h + 512, E5)
+            quant(cs, d, 768 * h + 512, 768 * h + 768, E5)
+
+        def XT(n, a, j, e):
+            t = bank(n, "xt%d" % a, [P, 4, P], tps, "tp")
+            words = x_raw(n)[:].rearrange("p a b q -> p (a b q)").bitcast(F32)
+            for i in range(4):
+                nc.tensor.transpose(t[:, i, :], words[:, 512 * a + i : 512 * a + 512 : 4], ident[:])
+
+        def XC(n, a, j, e):
+            t = tiles[n, "xt%d" % a]
+            src = t[:].rearrange("p t c -> p (t c)").bitcast(BF16).rearrange("p (t c r) -> p r c t", t=4, r=2)
+            copy(e)(out=x_grp(n)[:, 0:2, a], in_=src)
+
+        def XQ(n, ri, j, e):
+            quant(codes(n, "x", 1536, 2), x_grp(n)[:].rearrange("p s a m t -> p (s a m t)"), 512 * ri, 512 * ri + 512, E4)
+
+        def XN(n, i, j, e):
+            g = x_grp(n)[:].rearrange("p s a m t -> p s (a m t)")
+            nc.vector.tensor_scalar_mul(out=g[:, 2], in0=g[:, 1], scalar1=-1.0)
+
+        def XNQ(n, i, j, e):
+            quant(codes(n, "x", 1536, 2), x_grp(n)[:].rearrange("p s a m t -> p (s a m t)"), 1024, 1536, E4)
+
+        def O1(n, r, a, e):
+            t = bank(n, "o1%d%d" % (r, a), [P, BS], mps, "mm")
+            xc, dc = codes(n, "x", 1536, 2), codes(n, "dp", 1024, 2)
+            pairs = ((0, 0), (512, 512)) if r == 0 else ((0, 512), (1024, 0))
+            for i, (xlo, dlo) in enumerate(pairs):
+                mm(t[:], xc, xlo + 128 * a, E4, dc, dlo, E5, i == 0, i == 1)
+
+        def E1(n, r, a, e):
+            t = tiles[n, "o1%d%d" % (r, a)]
+            o = out_tile(n, "O1%d%d" % (r, a // 2), [P, 2, BS])
+            copy(e)(
+                out=o[:, a % 2].rearrange("p (k u e) -> p k u e", u=2, e=2),
+                in_=t[:].rearrange("p (u k e) -> p k u e", u=2, e=2),
+            )
+
+        def F1(n, r, a, e):
+            nc.sync.dma_start(out=o1_hbm[r][n][:, a : a + 2], in_=tiles[n, "O1%d%d" % (r, a // 2)][:])
+
+        def O0(n, h, a, e):
+            t = bank(n, "o0%d%d" % (h, a), [P, BS], mps, "mm")
+            wc, dc = codes(n, "w1", 1024, 2), codes(n, "dk", 1536, 2)
+            mm(t[:], wc, 128 * a, E4, dc, 768 * h, E5, True, False)
+            mm(t[:], wc, 512 + 128 * a, E4, dc, 768 * h + 256, E5, False, True)
+
+        def E0(n, h, a, e):
+            t = tiles[n, "o0%d%d" % (h, a)]
+            o = out_tile(n, "O0%d%d" % (h, a // 2), [P, 2, 2, 256])
+            copy(e)(
+                out=o[:, :, a % 2].rearrange("p b (q r) -> p b q r", r=2),
+                in_=t[:].rearrange("p (r b q) -> p b q r", r=2, b=2),
+            )
+
+        def F0(n, h, a, e):
+            nc.sync.dma_start(
+                out=o0_hbm[n][:, 2 * h : 2 * h + 2, 256 * a : 256 * (a + 2)],
+                in_=tiles[n, "O0%d%d" % (h, a // 2)][:].rearrange("p b a q -> p b (a q)"),
+            )
+
+        plain = {
+            "Lg": Lg, "Lx": Lx, "Lw1": Lw1, "Lw2": Lw2, "Lz": Lz, "GC": GC, "GQ": GQ, "GN": GN, "GNQ": GNQ,
+            "S1": S1, "ST": ST, "DI": DI, "DPQ": DPQ, "DT": DT, "DC": DC, "DN": DN, "DKQ": DKQ, "XT": XT,
+            "XC": XC, "XQ": XQ, "XN": XN, "XNQ": XNQ, "O1": O1, "E1": E1, "F1": F1, "O0": O0, "E0": E0, "F0": F0,
+        }
+        ctx.enter_context(tc.manual_schedule())
+        for step in ORDER.split():
+            name, idx, n, e = step.split(":")
+            n = int(n)
+            ids = [int(c) for c in idx if c != "-"]
+            if name == "WT":
+                WT(n, idx[0], ids[1], ids[2])
+            elif name == "WC":
+                WC(n, idx[0], ids[1], ids[2], e)
+            elif name == "WQ":
+                WQ(n, idx[0], ids[1])
+            else:
+                ids = ids + [0, 0]
+                plain[name](n, ids[0], ids[1], e)

@@ -18,39 +18,40 @@ FLOPS = 12 * NB * 2 * BS * BS * BS
 BYTES = 4 * (2 * 1024 * 1024) + 4 * 1024 * 1024 + 8 * 1024 * 1024
 
 ORDER = """
-Lg:2:0:D Lg:0:0:D GC:20:0:V Lw2:1:0:D GC:00:0:V WT:210:0:P Lw2:0:0:D WT:211:0:P
-GC:30:0:V GC:10:0:V GN:-:0:V GC:21:0:V GQ:0:0:V WT:200:0:P GC:01:0:S WC:210:0:S
-WC:211:0:S WC:200:0:S GC:31:0:V WT:201:0:P WC:201:0:S Lw1:0:0:D WT:100:0:P WC:100:0:S
-Lw1:1:0:D WT:101:0:P GC:11:0:V Lz:0:0:D WT:111:0:P WC:101:0:S WQ:21:0:V WQ:20:0:V
-WT:110:0:P WC:110:0:S WC:111:0:S GQ:1:0:V S1:03:0:P GNQ:-:0:V Lg:0:1:D S1:00:0:P
-WQ:10:0:V S1:02:0:P ST:03:0:V GC:01:1:S GC:00:1:S ST:00:0:V S1:01:0:P Lg:2:1:D
-GC:30:1:S Lw2:1:1:D GC:11:1:V GC:21:1:S S1:10:0:P S1:11:0:P ST:01:0:V ST:02:0:V
-Lw2:0:1:D Lw1:1:1:D S1:12:0:P S1:13:0:P WT:210:1:P GC:31:1:V Lz:1:0:D WC:210:1:S
-GC:10:1:V WT:211:1:P WT:201:1:P WC:211:1:S WT:200:1:P GC:20:1:V WT:110:1:P WQ:11:0:V
-WC:201:1:S GN:-:1:V DI:01:0:V Lx:0:0:D WQ:21:1:V WT:111:1:P DT:01:0:P Lx:1:0:D
-GQ:1:1:V DT:00:0:P WC:200:1:S WQ:20:1:V GQ:0:1:V WC:110:1:S WC:111:1:S S1:00:1:P
-S1:03:1:P DC:00:0:S S1:01:1:P S1:02:1:P ST:10:0:V ST:11:0:V ST:12:0:V Lx:2:0:D
-DC:01:0:S Lx:3:0:D DI:00:0:S DT:10:0:P DC:10:0:S ST:13:0:V DN:-:0:V DT:11:0:P
-Lz:0:1:D DC:11:0:S XT:1:0:P GNQ:-:1:V Lz:1:1:D S1:13:1:P XC:1:0:S XT:0:0:P
-DI:10:0:S XT:3:0:P XT:2:0:P DPQ:0:0:V DI:11:0:V S1:11:1:P XC:3:0:S XC:0:0:S
-DKQ:1:0:V O0:13:0:P ST:00:1:V Lw1:0:1:D O0:10:0:P O0:11:0:P ST:03:1:V S1:12:1:P
-XC:2:0:S ST:01:1:V ST:02:1:V DT:01:1:P WT:100:1:P Lx:2:1:D ST:13:1:V ST:11:1:V
-DKQ:0:0:V DT:00:1:P ST:12:1:V E0:13:0:S O0:12:0:P E0:10:0:S WC:100:1:S E0:11:0:S
-S1:10:1:P XQ:0:0:V O0:03:0:P XN:-:0:V XQ:1:0:V Lx:3:1:D DPQ:1:0:V E0:12:0:S
-O0:00:0:P O0:01:0:P Lx:0:1:D Lx:1:1:D DC:01:1:V F0:12:0:D ST:10:1:V DC:00:1:S
-O0:02:0:P E0:03:0:S E0:00:0:S DT:11:1:P DC:11:1:S DN:-:1:V XNQ:-:0:V XT:3:1:P
-F0:10:0:D WT:101:1:P E0:02:0:S DT:10:1:P O1:13:0:P DI:10:1:V DI:01:1:V DI:00:1:V
-F0:02:0:D WQ:11:1:V WC:101:1:S WQ:10:1:V O1:12:0:P E0:01:0:S DC:10:1:V O1:01:0:P
-E1:13:0:S O1:00:0:P O1:11:0:P XC:3:1:S E1:12:0:S O1:02:0:P E1:01:0:S DI:11:1:V
-DKQ:1:1:V O1:03:0:P O1:10:0:P DKQ:0:1:V E1:11:0:V E1:02:0:S E1:10:0:V XT:2:1:P
-E1:03:0:S F0:00:0:D XT:1:1:P XC:1:1:V F1:12:0:D F1:02:0:D E1:00:0:S XC:2:1:S
-XT:0:1:P O0:02:1:P E0:02:1:V DPQ:1:1:V XC:0:1:S O0:03:1:P XQ:1:1:V E0:03:1:S
-O0:11:1:P O0:10:1:P E0:11:1:S F1:00:0:D F1:10:0:D DPQ:0:1:V E0:10:1:S O0:13:1:P
-E0:13:1:S O0:12:1:P F0:02:1:D E0:12:1:S O0:01:1:P F0:10:1:D O0:00:1:P F0:12:1:D
-XQ:0:1:V O1:00:1:P XN:-:1:V XNQ:-:1:V E0:01:1:S E0:00:1:S F0:00:1:D O1:01:1:P
-O1:11:1:P E1:00:1:V E1:01:1:S F1:00:1:D O1:10:1:P O1:03:1:P E1:11:1:V O1:02:1:P
-E1:02:1:V E1:10:1:S F1:10:1:D O1:12:1:P E1:12:1:V O1:13:1:P E1:03:1:S F1:02:1:D
-E1:13:1:S F1:12:1:D
+Lw2:1:0:D:0 Lw2:0:0:D:0 HD:-:0:P:7 Lg:2:0:D:0 WT:201:0:P:0 GC:21:0:V:0 GC:20:0:V:0 WT:200:0:P:0
+WC:200:0:S:0 WT:210:0:P:3 WC:201:0:S:0 Lg:0:0:D:0 GC:01:0:V:0 GC:00:0:V:0 Lg:1:0:D:0 GC:11:0:S:0
+WC:210:0:S:0 Lg:3:0:D:0 WT:211:0:P:2 Lw1:0:0:D:0 WT:100:0:P:0 GC:31:0:V:0 GC:30:0:V:0 WC:211:0:S:0
+GC:10:0:V:0 GQ:1:0:V:0 WQ:20:0:V:0 Lw1:1:0:D:0 Lz:0:0:D:0 Lg:2:1:D:0 WQ:21:0:V:0 WT:101:0:P:0
+GQ:0:0:V:0 WC:100:0:S:0 WT:111:0:P:2 Lw2:0:1:D:0 S1:01:0:P:0 GN:-:0:V:0 Lg:0:1:D:0 GNQ:-:0:V:0
+ST:01:0:V:0 Lz:1:0:D:0 GC:20:1:S:0 S1:03:0:P:0 ST:03:0:V:0 WC:101:0:S:0 S1:02:0:P:0 ST:02:0:V:0
+S1:12:0:P:0 S1:00:0:P:0 ST:00:0:V:0 S1:11:0:P:0 WC:111:0:S:0 WQ:10:0:V:0 WT:200:1:P:0 DI:01:0:V:0
+WT:201:1:P:0 Lw2:1:1:D:0 Lx:0:0:D:0 DI:00:0:V:0 GC:21:1:S:0 ST:11:0:V:0 DPQ:0:0:V:0 WC:200:1:S:0
+WC:201:1:S:0 Lx:1:0:D:0 Lx:3:0:D:0 S1:13:0:P:0 Lx:2:0:D:0 GC:01:1:V:0 DT:00:0:P:0 GC:00:1:S:0
+DC:00:0:S:0 DT:01:0:P:0 DC:01:0:S:0 WT:110:0:P:0 WC:110:0:S:0 ST:13:0:V:0 S1:10:0:P:0 WT:210:1:P:0
+ST:10:0:V:0 WC:210:1:S:0 WT:211:1:P:0 WC:211:1:S:0 ST:12:0:V:0 DT:10:0:P:1 DT:11:0:P:1 WQ:20:1:V:0
+DC:10:0:S:0 WQ:11:0:V:0 XT:1:0:P:0 XT:3:0:P:2 DC:11:0:S:0 DN:-:0:V:0 XT:2:0:P:0 DKQ:0:0:V:0
+O0:03:0:P:0 Lg:1:1:D:0 GC:11:1:V:0 Lg:3:1:D:0 O0:01:0:P:0 Lw1:1:1:D:0 O0:02:0:P:0 XT:0:0:P:0
+Lw1:0:1:D:0 WQ:21:1:V:0 WT:100:1:P:0 GC:10:1:S:0 XC:1:0:S:0 XC:3:0:S:0 GC:31:1:S:0 XC:2:0:S:0
+GC:30:1:V:0 DKQ:1:0:V:0 O0:10:0:P:0 O0:00:0:P:0 DI:11:0:V:0 XC:0:0:S:0 O0:11:0:P:0 WC:100:1:S:0
+Lz:0:1:D:0 E0:03:0:V:0 E0:01:0:S:0 GQ:1:1:V:0 E0:02:0:S:0 WT:101:1:P:0 WT:110:1:P:0 GN:-:1:V:0
+GQ:0:1:V:0 S1:03:1:P:0 Lx:3:1:D:0 XQ:0:0:V:0 E0:10:0:S:0 GNQ:-:1:V:0 XQ:1:0:V:0 S1:02:1:P:0
+XN:-:0:V:0 E0:00:0:S:0 ST:03:1:V:0 ST:02:1:V:0 S1:00:1:P:0 WC:101:1:S:0 S1:01:1:P:0 O0:13:0:P:0
+Lx:0:1:D:0 Lx:2:1:D:0 ST:00:1:V:0 Lz:1:1:D:0 Lx:1:1:D:0 ST:01:1:V:0 F0:00:0:D:0 E0:11:0:S:0
+S1:13:1:P:0 F0:02:0:D:0 XNQ:-:0:V:0 WC:110:1:S:0 DT:00:1:P:0 WT:111:1:P:0 DI:10:0:S:0 DPQ:1:0:V:0
+DT:01:1:P:0 ST:13:1:V:0 E0:13:0:S:0 S1:12:1:P:0 DI:00:1:V:0 DC:00:1:S:0 O0:12:0:P:0 O1:03:0:P:0
+S1:11:1:P:0 S1:10:1:P:0 O1:02:0:P:0 DC:01:1:S:0 WC:111:1:S:0 E0:12:0:S:0 F0:12:0:D:0 O1:13:0:P:0
+E1:03:0:S:0 ST:12:1:V:0 DT:11:1:P:0 DI:01:1:S:0 WQ:11:1:V:0 E1:02:0:S:0 F1:02:0:D:0 DN:-:1:V:0
+WQ:10:1:V:0 XT:3:1:P:0 XT:1:1:P:0 ST:10:1:V:0 DC:11:1:S:0 ST:11:1:V:0 E1:13:0:V:0 DPQ:0:1:V:0
+DT:10:1:P:0 DI:11:1:V:0 DC:10:1:V:0 XC:3:1:S:0 O1:12:0:P:0 E1:12:0:S:0 O1:00:0:P:0 XC:1:1:S:0
+O1:01:0:P:0 O1:11:0:P:0 DI:10:1:V:0 O1:10:0:P:0 DKQ:1:1:V:0 E1:00:0:S:0 F1:12:0:D:0 E1:01:0:S:0
+F0:10:0:D:0 E1:11:0:S:0 DKQ:0:1:V:0 F1:00:0:D:0 XT:0:1:P:0 XT:2:1:P:0 XC:2:1:S:0 O0:10:1:P:0
+E1:10:0:V:0 F1:10:0:D:0 O0:11:1:P:0 XC:0:1:V:0 O0:00:1:P:0 E0:11:1:S:0 E0:00:1:S:0 O0:01:1:P:0
+E0:10:1:V:0 O0:12:1:P:0 O0:13:1:P:0 XQ:0:1:V:0 DPQ:1:1:V:0 F0:10:1:D:0 E0:01:1:S:0 XQ:1:1:V:0
+O1:01:1:P:0 O1:00:1:P:0 F0:00:1:D:0 XN:-:1:V:0 XNQ:-:1:V:0 E0:12:1:S:0 E0:13:1:S:0 F0:12:1:D:0
+E1:00:1:V:0 O1:03:1:P:0 O1:02:1:P:0 E1:01:1:S:0 F1:01:1:D:0 F1:00:1:D:0 O1:13:1:P:0 E1:02:1:S:0
+O1:12:1:P:0 E1:03:1:V:0 F1:03:1:D:0 O1:11:1:P:0 F1:02:1:D:0 E1:13:1:S:0 F1:13:1:D:0 E1:12:1:S:0
+F1:12:1:D:0 O1:10:1:P:0 E1:10:1:S:0 O0:03:1:P:0 E0:03:1:S:0 E1:11:1:V:0 F1:11:1:D:0 O0:02:1:P:0
+E0:02:1:S:0 F1:10:1:D:0 F0:02:1:D:0
 """
 T_BANKS = 3
 M_BANKS = 5
@@ -77,6 +78,16 @@ def tile_scatteringmodule_pa_v_kernel(tc, xh, w1, w2, b1, b2, z1, grad_out, out_
 
         ident = const.tile([P, P], F32, name="ident")
         make_identity(nc, ident[:])
+        zeros = const.tile([P, BS], BF16, name="zeros")
+        nc.gpsimd.memset(zeros[:], 0.0)
+
+        def warm(t, count):
+            for i in range(count):
+                nc.tensor.matmul(t, lhsT=zeros[:, 0:P], rhs=zeros[:], start=True, stop=True)
+
+        def HD(n, i, j, e):
+            t = mps.tile([P, BS], F32, name="mm", tag="mm")
+            warm(t[:], i)
 
         def quant(cs, grouped, lo, hi, fmt):
             nc.vector.quantize_mx(
@@ -150,9 +161,7 @@ def tile_scatteringmodule_pa_v_kernel(tc, xh, w1, w2, b1, b2, z1, grad_out, out_
             return tiles[n, key]
 
         def Lg(n, b, j, e):
-            nc.sync.dma_start(
-                out=g_raw(n)[:, b : b + 2].rearrange("p b t q -> p b (t q)"), in_=g_hbm[n][:, b : b + 2, :]
-            )
+            nc.sync.dma_start(out=g_raw(n)[:, b].rearrange("p t q -> p (t q)"), in_=g_hbm[n][:, b, :])
 
         def Lx(n, b, j, e):
             nc.sync.dma_start(out=x_raw(n)[:, :, b, :], in_=x_hbm[n][:, b, :].rearrange("p (a q) -> p a q", a=4))
@@ -181,9 +190,10 @@ def tile_scatteringmodule_pa_v_kernel(tc, xh, w1, w2, b1, b2, z1, grad_out, out_
         def GNQ(n, i, j, e):
             quant(codes(n, "g", 1536), g_grp(n)[:].rearrange("p s j m t -> p (s j m t)"), 1024, 1536, E5)
 
-        def WT(n, k, r, half):
+        def WT(n, k, r, half, d):
             words = w_raw(n, k, r)[:].rearrange("p a k -> p (a k)").bitcast(F32)
             t = bank(n, "wt%s%d%d" % (k, r, half), [P, 2, 2, P], tps, "tp")
+            warm(t[:].rearrange("p a u m -> p (a u m)"), d)
             for a in range(2):
                 for u in range(2):
                     lo = (2 * half + a) * 256 + u
@@ -230,6 +240,7 @@ def tile_scatteringmodule_pa_v_kernel(tc, xh, w1, w2, b1, b2, z1, grad_out, out_
         def DT(n, r, u, e):
             words = dz_tile(n, r)[:].rearrange("p t k -> p (t k)").bitcast(F32)
             t = bank(n, "dt%d%d" % (r, u), [P, 2, 2, P], tps, "tp")
+            warm(t[:].rearrange("p a u m -> p (a u m)"), e)
             for i in range(2):
                 for v in range(2):
                     lo = (2 * u + i) * 256 + v * 128
@@ -254,6 +265,7 @@ def tile_scatteringmodule_pa_v_kernel(tc, xh, w1, w2, b1, b2, z1, grad_out, out_
 
         def XT(n, a, j, e):
             t = bank(n, "xt%d" % a, [P, 4, P], tps, "tp")
+            warm(t[:].rearrange("p t c -> p (t c)"), e)
             words = x_raw(n)[:].rearrange("p a b q -> p (a b q)").bitcast(F32)
             for i in range(4):
                 nc.tensor.transpose(t[:, i, :], words[:, 512 * a + i : 512 * a + 512 : 4], ident[:])
@@ -289,7 +301,10 @@ def tile_scatteringmodule_pa_v_kernel(tc, xh, w1, w2, b1, b2, z1, grad_out, out_
             )
 
         def F1(n, r, a, e):
-            nc.sync.dma_start(out=o1_hbm[r][n][:, a : a + 2], in_=tiles[n, "O1%d%d" % (r, a // 2)][:])
+            w = 2 - n
+            nc.sync.dma_start(
+                out=o1_hbm[r][n][:, a : a + w], in_=tiles[n, "O1%d%d" % (r, a // 2)][:, a % 2 : a % 2 + w]
+            )
 
         def O0(n, h, a, e):
             t = bank(n, "o0%d%d" % (h, a), [P, BS], mps, "mm")
@@ -312,21 +327,24 @@ def tile_scatteringmodule_pa_v_kernel(tc, xh, w1, w2, b1, b2, z1, grad_out, out_
             )
 
         plain = {
-            "Lg": Lg, "Lx": Lx, "Lw1": Lw1, "Lw2": Lw2, "Lz": Lz, "GC": GC, "GQ": GQ, "GN": GN, "GNQ": GNQ,
+            "HD": HD, "Lg": Lg, "Lx": Lx, "Lw1": Lw1, "Lw2": Lw2, "Lz": Lz, "GC": GC, "GQ": GQ, "GN": GN, "GNQ": GNQ,
             "S1": S1, "ST": ST, "DI": DI, "DPQ": DPQ, "DT": DT, "DC": DC, "DN": DN, "DKQ": DKQ, "XT": XT,
             "XC": XC, "XQ": XQ, "XN": XN, "XNQ": XNQ, "O1": O1, "E1": E1, "F1": F1, "O0": O0, "E0": E0, "F0": F0,
         }
         ctx.enter_context(tc.manual_schedule())
         for step in ORDER.split():
-            name, idx, n, e = step.split(":")
+            name, idx, n, e, d = step.split(":")
             n = int(n)
+            d = int(d)
             ids = [int(c) for c in idx if c != "-"]
-            if name == "WT":
-                WT(n, idx[0], ids[1], ids[2])
+            if name == "HD":
+                HD(n, d, 0, e)
+            elif name == "WT":
+                WT(n, idx[0], ids[1], ids[2], d)
             elif name == "WC":
                 WC(n, idx[0], ids[1], ids[2], e)
             elif name == "WQ":
                 WQ(n, idx[0], ids[1])
             else:
                 ids = ids + [0, 0]
-                plain[name](n, ids[0], ids[1], e)
+                plain[name](n, ids[0], ids[1], d if e == "P" else e)

@@ -18,44 +18,44 @@ FLOPS = 12 * NB * 2 * BS * BS * BS
 BYTES = 4 * (2 * 1024 * 1024) + 4 * 1024 * 1024 + 8 * 1024 * 1024
 
 ORDER = """
-Lw2:1:0:D:0 Lw2:0:0:D:0 HD:-:0:P:7 Lg:2:0:D:0 WT:201:0:P:0 GC:21:0:V:0 GC:20:0:V:0 WT:200:0:P:0
-WC:200:0:S:0 WT:210:0:P:3 WC:201:0:S:0 Lg:0:0:D:0 GC:01:0:V:0 GC:00:0:V:0 Lg:1:0:D:0 GC:11:0:S:0
-WC:210:0:S:0 Lg:3:0:D:0 WT:211:0:P:2 Lw1:0:0:D:0 WT:100:0:P:0 GC:31:0:V:0 GC:30:0:V:0 WC:211:0:S:0
-GC:10:0:V:0 GQ:1:0:V:0 WQ:20:0:V:0 Lw1:1:0:D:0 Lz:0:0:D:0 Lg:2:1:D:0 WQ:21:0:V:0 WT:101:0:P:0
-GQ:0:0:V:0 WC:100:0:S:0 WT:111:0:P:2 Lw2:0:1:D:0 S1:01:0:P:0 GN:-:0:V:0 Lg:0:1:D:0 GNQ:-:0:V:0
-ST:01:0:V:0 Lz:1:0:D:0 GC:20:1:S:0 S1:03:0:P:0 ST:03:0:V:0 WC:101:0:S:0 S1:02:0:P:0 ST:02:0:V:0
-S1:12:0:P:0 S1:00:0:P:0 ST:00:0:V:0 S1:11:0:P:0 WC:111:0:S:0 WQ:10:0:V:0 WT:200:1:P:0 DI:01:0:V:0
-WT:201:1:P:0 Lw2:1:1:D:0 Lx:0:0:D:0 DI:00:0:V:0 GC:21:1:S:0 ST:11:0:V:0 DPQ:0:0:V:0 WC:200:1:S:0
-WC:201:1:S:0 Lx:1:0:D:0 Lx:3:0:D:0 S1:13:0:P:0 Lx:2:0:D:0 GC:01:1:V:0 DT:00:0:P:0 GC:00:1:S:0
-DC:00:0:S:0 DT:01:0:P:0 DC:01:0:S:0 WT:110:0:P:0 WC:110:0:S:0 ST:13:0:V:0 S1:10:0:P:0 WT:210:1:P:0
-ST:10:0:V:0 WC:210:1:S:0 WT:211:1:P:0 WC:211:1:S:0 ST:12:0:V:0 DT:10:0:P:1 DT:11:0:P:1 WQ:20:1:V:0
-DC:10:0:S:0 WQ:11:0:V:0 XT:1:0:P:0 XT:3:0:P:2 DC:11:0:S:0 DN:-:0:V:0 XT:2:0:P:0 DKQ:0:0:V:0
-O0:03:0:P:0 Lg:1:1:D:0 GC:11:1:V:0 Lg:3:1:D:0 O0:01:0:P:0 Lw1:1:1:D:0 O0:02:0:P:0 XT:0:0:P:0
-Lw1:0:1:D:0 WQ:21:1:V:0 WT:100:1:P:0 GC:10:1:S:0 XC:1:0:S:0 XC:3:0:S:0 GC:31:1:S:0 XC:2:0:S:0
-GC:30:1:V:0 DKQ:1:0:V:0 O0:10:0:P:0 O0:00:0:P:0 DI:11:0:V:0 XC:0:0:S:0 O0:11:0:P:0 WC:100:1:S:0
-Lz:0:1:D:0 E0:03:0:V:0 E0:01:0:S:0 GQ:1:1:V:0 E0:02:0:S:0 WT:101:1:P:0 WT:110:1:P:0 GN:-:1:V:0
-GQ:0:1:V:0 S1:03:1:P:0 Lx:3:1:D:0 XQ:0:0:V:0 E0:10:0:S:0 GNQ:-:1:V:0 XQ:1:0:V:0 S1:02:1:P:0
-XN:-:0:V:0 E0:00:0:S:0 ST:03:1:V:0 ST:02:1:V:0 S1:00:1:P:0 WC:101:1:S:0 S1:01:1:P:0 O0:13:0:P:0
-Lx:0:1:D:0 Lx:2:1:D:0 ST:00:1:V:0 Lz:1:1:D:0 Lx:1:1:D:0 ST:01:1:V:0 F0:00:0:D:0 E0:11:0:S:0
-S1:13:1:P:0 F0:02:0:D:0 XNQ:-:0:V:0 WC:110:1:S:0 DT:00:1:P:0 WT:111:1:P:0 DI:10:0:S:0 DPQ:1:0:V:0
-DT:01:1:P:0 ST:13:1:V:0 E0:13:0:S:0 S1:12:1:P:0 DI:00:1:V:0 DC:00:1:S:0 O0:12:0:P:0 O1:03:0:P:0
-S1:11:1:P:0 S1:10:1:P:0 O1:02:0:P:0 DC:01:1:S:0 WC:111:1:S:0 E0:12:0:S:0 F0:12:0:D:0 O1:13:0:P:0
-E1:03:0:S:0 ST:12:1:V:0 DT:11:1:P:0 DI:01:1:S:0 WQ:11:1:V:0 E1:02:0:S:0 F1:02:0:D:0 DN:-:1:V:0
-WQ:10:1:V:0 XT:3:1:P:0 XT:1:1:P:0 ST:10:1:V:0 DC:11:1:S:0 ST:11:1:V:0 E1:13:0:V:0 DPQ:0:1:V:0
-DT:10:1:P:0 DI:11:1:V:0 DC:10:1:V:0 XC:3:1:S:0 O1:12:0:P:0 E1:12:0:S:0 O1:00:0:P:0 XC:1:1:S:0
-O1:01:0:P:0 O1:11:0:P:0 DI:10:1:V:0 O1:10:0:P:0 DKQ:1:1:V:0 E1:00:0:S:0 F1:12:0:D:0 E1:01:0:S:0
-F0:10:0:D:0 E1:11:0:S:0 DKQ:0:1:V:0 F1:00:0:D:0 XT:0:1:P:0 XT:2:1:P:0 XC:2:1:S:0 O0:10:1:P:0
-E1:10:0:V:0 F1:10:0:D:0 O0:11:1:P:0 XC:0:1:V:0 O0:00:1:P:0 E0:11:1:S:0 E0:00:1:S:0 O0:01:1:P:0
-E0:10:1:V:0 O0:12:1:P:0 O0:13:1:P:0 XQ:0:1:V:0 DPQ:1:1:V:0 F0:10:1:D:0 E0:01:1:S:0 XQ:1:1:V:0
-O1:01:1:P:0 O1:00:1:P:0 F0:00:1:D:0 XN:-:1:V:0 XNQ:-:1:V:0 E0:12:1:S:0 E0:13:1:S:0 F0:12:1:D:0
-E1:00:1:V:0 O1:03:1:P:0 O1:02:1:P:0 E1:01:1:S:0 F1:01:1:D:0 F1:00:1:D:0 O1:13:1:P:0 E1:02:1:S:0
-O1:12:1:P:0 E1:03:1:V:0 F1:03:1:D:0 O1:11:1:P:0 F1:02:1:D:0 E1:13:1:S:0 F1:13:1:D:0 E1:12:1:S:0
-F1:12:1:D:0 O1:10:1:P:0 E1:10:1:S:0 O0:03:1:P:0 E0:03:1:S:0 E1:11:1:V:0 F1:11:1:D:0 O0:02:1:P:0
-E0:02:1:S:0 F1:10:1:D:0 F0:02:1:D:0
+HD:-:0:P:5 Lw2:0:0:D:0 WT:200:0:P:0 Lg:0:0:D:0 GC:00:0:V:0 Lw2:1:0:D:0 Lg:1:0:D:0 Lg:2:0:D:0
+WC:200:0:S:0 Lg:3:0:D:0 GC:01:0:S:0 GC:10:0:V:0 WT:201:0:P:0 GC:11:0:V:0 GC:20:0:V:0 WC:201:0:S:0
+GC:21:0:S:0 GC:30:0:S:0 WT:210:0:P:2 WT:211:0:P:4 WQ:20:0:V:0 GC:31:0:S:0 Lw1:0:0:D:0 WT:100:0:P:3
+WC:210:0:V:0 WC:211:0:S:0 WT:101:0:P:0 GN:-:0:V:0 Lw1:1:0:D:0 GQ:0:0:V:0 WT:110:0:P:0 WT:111:0:P:0
+GQ:1:0:V:0 WQ:21:0:V:0 S1:00:0:P:0 Lz:0:0:D:0 WC:100:0:S:0 S1:01:0:P:0 GNQ:-:0:V:0 WC:101:0:S:0
+WQ:10:0:V:0 WC:110:0:S:0 Lg:0:1:D:0 ST:00:0:V:0 S1:02:0:P:0 ST:01:0:V:0 S1:03:0:P:0 Lz:1:0:D:0
+Lw2:0:1:D:0 ST:02:0:V:0 S1:10:0:P:0 S1:11:0:P:0 S1:12:0:P:0 ST:03:0:V:0 DT:00:0:P:0 Lw2:1:1:D:0
+WC:111:0:S:0 WT:200:1:P:0 Lx:0:0:D:0 GC:00:1:S:0 ST:10:0:V:0 DI:00:0:V:0 WT:201:1:P:0 DT:01:0:P:0
+GC:01:1:S:0 WQ:11:0:V:0 DI:01:0:S:0 DPQ:0:0:V:0 S1:13:0:P:0 DC:00:0:S:0 WC:200:1:S:0 ST:11:0:V:0
+ST:12:0:V:0 WT:210:1:P:0 Lx:1:0:D:0 WC:201:1:S:0 Lx:2:0:D:0 DT:10:0:P:0 ST:13:0:V:0 WQ:20:1:V:0
+DC:01:0:S:0 WT:211:1:P:1 DN:-:0:V:0 WC:210:1:S:0 DC:10:0:S:0 Lx:3:0:D:0 Lg:1:1:D:0 DT:11:0:P:1
+WC:211:1:V:0 Lg:2:1:D:0 XT:0:0:P:0 XT:1:0:P:0 GC:10:1:V:0 XT:2:0:P:2 GC:11:1:V:0 XT:3:0:P:0
+DC:11:0:S:0 XC:0:0:S:0 DKQ:0:0:V:0 O0:00:0:P:0 WQ:21:1:V:0 O0:01:0:P:0 Lg:3:1:D:0 Lw1:0:1:D:0
+XC:1:0:S:0 Lw1:1:1:D:0 DKQ:1:0:V:0 GC:20:1:S:0 GC:21:1:V:0 GC:30:1:V:0 O0:10:0:P:0 O0:11:0:P:0
+GC:31:1:V:0 XC:2:0:S:0 GQ:0:1:V:0 XC:3:0:S:0 E0:00:0:V:0 GQ:1:1:V:0 E0:01:0:S:0 WT:100:1:P:0
+E0:10:0:S:0 GN:-:1:V:0 WT:101:1:P:0 O0:02:0:P:0 S1:00:1:P:0 E0:11:0:S:0 XQ:0:0:V:0 S1:01:1:P:0
+Lz:0:1:D:0 Lx:0:1:D:0 O0:03:0:P:0 E0:02:0:S:0 XN:-:0:V:0 Lx:1:1:D:0 GNQ:-:1:V:0 ST:00:1:V:0
+WC:100:1:S:0 ST:01:1:V:0 DI:10:0:S:0 E0:03:0:V:0 O0:12:0:P:0 Lx:2:1:D:0 S1:02:1:P:0 DI:11:0:S:0
+S1:10:1:P:0 WC:101:1:S:0 ST:02:1:V:0 E0:12:0:S:0 XQ:1:0:V:0 Lx:3:1:D:0 S1:03:1:P:0 WT:110:1:P:0
+DT:00:1:P:0 WC:110:1:S:0 DC:00:1:S:0 ST:03:1:V:0 WT:111:1:P:0 WC:111:1:S:0 S1:11:1:P:0 Lz:1:1:D:0
+ST:10:1:V:0 DPQ:1:0:V:0 DI:00:1:S:0 S1:12:1:P:0 S1:13:1:P:0 XNQ:-:0:V:0 O1:10:0:P:0 ST:11:1:V:0
+O1:00:0:P:0 ST:12:1:V:0 O1:11:0:P:0 E1:10:0:S:0 E1:00:0:S:0 E1:11:0:S:0 O1:12:0:P:0 E1:12:0:S:0
+F0:00:0:D:0 ST:13:1:V:0 O1:01:0:P:0 E1:01:0:S:0 WQ:10:1:V:0 WQ:11:1:V:0 DT:01:1:P:0 DT:10:1:P:0
+DI:10:1:V:0 DI:01:1:V:0 DI:11:1:V:0 DC:01:1:S:0 DC:10:1:S:0 DT:11:1:P:0 O0:13:0:P:0 DPQ:0:1:V:0
+DN:-:1:V:0 O1:02:0:P:0 O1:03:0:P:0 O1:13:0:P:0 E1:02:0:V:0 E0:13:0:S:0 DC:11:1:S:0 DKQ:0:1:V:0
+XT:0:1:P:0 XT:1:1:P:0 DPQ:1:1:V:0 DKQ:1:1:V:0 E1:03:0:S:0 E1:13:0:S:0 F1:10:0:D:0 O0:00:1:P:0
+XC:0:1:S:0 XC:1:1:S:0 O0:01:1:P:0 XT:2:1:P:0 F1:00:0:D:0 XT:3:1:P:0 O0:10:1:P:0 XC:2:1:S:0
+F0:10:0:D:0 E0:10:1:S:0 O0:11:1:P:0 E0:00:1:V:0 E0:11:1:S:0 E0:01:1:V:0 O0:12:1:P:0 XC:3:1:V:0
+XQ:0:1:V:0 F1:12:0:D:0 O0:13:1:P:0 F1:02:0:D:0 XN:-:1:V:0 F0:00:1:D:0 F0:10:1:D:0 E0:12:1:S:0
+XQ:1:1:V:0 O0:02:1:P:0 E0:13:1:S:0 XNQ:-:1:V:0 O0:03:1:P:0 O1:00:1:P:0 E0:02:1:V:0 O1:01:1:P:0
+E0:03:1:S:0 O1:02:1:P:0 E1:00:1:S:0 O1:03:1:P:0 F0:12:1:D:0 F0:02:1:D:0 O1:10:1:P:0 E1:01:1:V:0
+F1:00:1:D:0 O1:11:1:P:0 E1:02:1:S:0 F1:01:1:D:0 E1:10:1:V:0 O1:12:1:P:0 E1:03:1:S:0 F1:02:1:D:0
+F1:03:1:D:0 E1:11:1:S:0 E1:12:1:V:0 O1:13:1:P:0 E1:13:1:S:0 F1:10:1:D:0 F1:11:1:D:0 F1:12:1:D:0
+F1:13:1:D:0
 """
 T_BANKS = 3
 M_BANKS = 5
-OUT_BUFS = 10
+OUT_BUFS = 8
 
 
 def tile_scatteringmodule_pa_v_kernel(tc, xh, w1, w2, b1, b2, z1, grad_out, out_0, out_1):
@@ -154,9 +154,9 @@ def tile_scatteringmodule_pa_v_kernel(tc, xh, w1, w2, b1, b2, z1, grad_out, out_
         def x_grp(n):
             return get(n, "x_grp", [P, 3, 4, P, 4], BF16, grp)
 
-        def out_tile(n, key, shape):
+        def out_tile(n, key, shape, tag, bufs):
             if (n, key) not in tiles:
-                t = outs.tile(shape, F32, name="o", tag="o")
+                t = outs.tile(shape, F32, name=tag, tag=tag, bufs=bufs)
                 tiles[n, key] = t
             return tiles[n, key]
 
@@ -294,7 +294,7 @@ def tile_scatteringmodule_pa_v_kernel(tc, xh, w1, w2, b1, b2, z1, grad_out, out_
 
         def E1(n, r, a, e):
             t = tiles[n, "o1%d%d" % (r, a)]
-            o = out_tile(n, "O1%d%d" % (r, a // 2), [P, 2, BS])
+            o = out_tile(n, "O1%d%d" % (r, a // 2), [P, 2, BS], "o2", OUT_BUFS)
             copy(e)(
                 out=o[:, a % 2].rearrange("p (k u e) -> p k u e", u=2, e=2),
                 in_=t[:].rearrange("p (u k e) -> p k u e", u=2, e=2),
@@ -314,16 +314,18 @@ def tile_scatteringmodule_pa_v_kernel(tc, xh, w1, w2, b1, b2, z1, grad_out, out_
 
         def E0(n, h, a, e):
             t = tiles[n, "o0%d%d" % (h, a)]
-            o = out_tile(n, "O0%d%d" % (h, a // 2), [P, 2, 2, 256])
+            w = 4 - 2 * n
+            o = out_tile(n, "O0%d%d" % (h, a // w), [P, 2, w, 256], "o%d" % w, 2 if w == 4 else OUT_BUFS)
             copy(e)(
-                out=o[:, :, a % 2].rearrange("p b (q r) -> p b q r", r=2),
+                out=o[:, :, a % w].rearrange("p b (q r) -> p b q r", r=2),
                 in_=t[:].rearrange("p (r b q) -> p b q r", r=2, b=2),
             )
 
         def F0(n, h, a, e):
+            w = 4 - 2 * n
             nc.sync.dma_start(
-                out=o0_hbm[n][:, 2 * h : 2 * h + 2, 256 * a : 256 * (a + 2)],
-                in_=tiles[n, "O0%d%d" % (h, a // 2)][:].rearrange("p b a q -> p b (a q)"),
+                out=o0_hbm[n][:, 2 * h : 2 * h + 2, 256 * a : 256 * (a + w)],
+                in_=tiles[n, "O0%d%d" % (h, a // w)][:].rearrange("p b a q -> p b (a q)"),
             )
 
         plain = {

@@ -7,346 +7,425 @@ F32 = mybir.dt.float32
 BF16 = mybir.dt.bfloat16
 U32 = mybir.dt.uint32
 U8 = mybir.dt.uint8
-E4 = mybir.dt.float8_e4m3fn_x4
-E5 = mybir.dt.float8_e5m2_x4
+E4M3 = mybir.dt.float8_e4m3fn_x4
+E5M2 = mybir.dt.float8_e5m2_x4
 ALU = mybir.AluOpType
 
 P = 128
 NB = 2
 BS = 512
+BATCH = 4
+ROW = 256
+PACK = 4
 FLOPS = 12 * NB * 2 * BS * BS * BS
-BYTES = 4 * (2 * 1024 * 1024) + 4 * 1024 * 1024 + 8 * 1024 * 1024
+BYTES = 2 * (4 * NB * 2 * BS * BS) + 4 * (3 * NB * 2 * BS * BS)
+
+RE, IM, NEG = 0, 1, 2
+
+TURN_BANKS = 3
+MUL_BANKS = 8 - TURN_BANKS
+OUT_BUFS = 8
+
+TILES = {
+    "g_raw": ((BATCH, PACK, ROW), BF16, 1),
+    "x_raw": ((4, BATCH, ROW), BF16, 1),
+    "w1_raw0": ((4, BS), BF16, 1),
+    "w1_raw1": ((4, BS), BF16, 1),
+    "w2_raw0": ((4, BS), BF16, 1),
+    "w2_raw1": ((4, BS), BF16, 1),
+    "z_raw0": ((4, BS), F32, 1),
+    "z_raw1": ((4, BS), F32, 1),
+    "g_words": ((3, 4, P, PACK), BF16, 1),
+    "w1_words": ((2, 4, P, PACK), BF16, 1),
+    "w2_words": ((2, 4, P, PACK), BF16, 1),
+    "x_words": ((3, 4, P, PACK), BF16, 1),
+    "dz0": ((4, BS), BF16, 1),
+    "dz1": ((4, BS), BF16, 1),
+    "dzp_words": ((2, BS, PACK), BF16, 1),
+    "dzk_words": ((2, 3, ROW, PACK), BF16, 1),
+    "g_codes": ((3 * BS,), U32, 1),
+    "g_scales": ((3 * BS,), U8, 1),
+    "w1_codes": ((2 * BS,), U32, 2),
+    "w1_scales": ((2 * BS,), U8, 2),
+    "w2_codes": ((2 * BS,), U32, 1),
+    "w2_scales": ((2 * BS,), U8, 1),
+    "x_codes": ((3 * BS,), U32, 2),
+    "x_scales": ((3 * BS,), U8, 2),
+    "dzp_codes": ((2 * BS,), U32, 2),
+    "dzp_scales": ((2 * BS,), U8, 2),
+    "dzk_codes": ((6 * ROW,), U32, 2),
+    "dzk_scales": ((6 * ROW,), U8, 2),
+}
 
 ORDER = """
-HD:-:0:P:5 Lw2:0:0:D:0 WT:200:0:P:0 Lg:0:0:D:0 GC:00:0:V:0 Lw2:1:0:D:0 Lg:1:0:D:0 Lg:2:0:D:0
-WC:200:0:S:0 Lg:3:0:D:0 GC:01:0:S:0 GC:10:0:V:0 WT:201:0:P:0 GC:11:0:V:0 GC:20:0:V:0 WC:201:0:S:0
-GC:21:0:S:0 GC:30:0:S:0 WT:210:0:P:2 WT:211:0:P:4 WQ:20:0:V:0 GC:31:0:S:0 Lw1:0:0:D:0 WT:100:0:P:3
-WC:210:0:V:0 WC:211:0:S:0 WT:101:0:P:0 GN:-:0:V:0 Lw1:1:0:D:0 GQ:0:0:V:0 WT:110:0:P:0 WT:111:0:P:0
-GQ:1:0:V:0 WQ:21:0:V:0 S1:00:0:P:0 Lz:0:0:D:0 WC:100:0:S:0 S1:01:0:P:0 GNQ:-:0:V:0 WC:101:0:S:0
-WQ:10:0:V:0 WC:110:0:S:0 Lg:0:1:D:0 ST:00:0:V:0 S1:02:0:P:0 ST:01:0:V:0 S1:03:0:P:0 Lz:1:0:D:0
-Lw2:0:1:D:0 ST:02:0:V:0 S1:10:0:P:0 S1:11:0:P:0 S1:12:0:P:0 ST:03:0:V:0 DT:00:0:P:0 Lw2:1:1:D:0
-WC:111:0:S:0 WT:200:1:P:0 Lx:0:0:D:0 GC:00:1:S:0 ST:10:0:V:0 DI:00:0:V:0 WT:201:1:P:0 DT:01:0:P:0
-GC:01:1:S:0 WQ:11:0:V:0 DI:01:0:S:0 DPQ:0:0:V:0 S1:13:0:P:0 DC:00:0:S:0 WC:200:1:S:0 ST:11:0:V:0
-ST:12:0:V:0 WT:210:1:P:0 Lx:1:0:D:0 WC:201:1:S:0 Lx:2:0:D:0 DT:10:0:P:0 ST:13:0:V:0 WQ:20:1:V:0
-DC:01:0:S:0 WT:211:1:P:1 DN:-:0:V:0 WC:210:1:S:0 DC:10:0:S:0 Lx:3:0:D:0 Lg:1:1:D:0 DT:11:0:P:1
-WC:211:1:V:0 Lg:2:1:D:0 XT:0:0:P:0 XT:1:0:P:0 GC:10:1:V:0 XT:2:0:P:2 GC:11:1:V:0 XT:3:0:P:0
-DC:11:0:S:0 XC:0:0:S:0 DKQ:0:0:V:0 O0:00:0:P:0 WQ:21:1:V:0 O0:01:0:P:0 Lg:3:1:D:0 Lw1:0:1:D:0
-XC:1:0:S:0 Lw1:1:1:D:0 DKQ:1:0:V:0 GC:20:1:S:0 GC:21:1:V:0 GC:30:1:V:0 O0:10:0:P:0 O0:11:0:P:0
-GC:31:1:V:0 XC:2:0:S:0 GQ:0:1:V:0 XC:3:0:S:0 E0:00:0:V:0 GQ:1:1:V:0 E0:01:0:S:0 WT:100:1:P:0
-E0:10:0:S:0 GN:-:1:V:0 WT:101:1:P:0 O0:02:0:P:0 S1:00:1:P:0 E0:11:0:S:0 XQ:0:0:V:0 S1:01:1:P:0
-Lz:0:1:D:0 Lx:0:1:D:0 O0:03:0:P:0 E0:02:0:S:0 XN:-:0:V:0 Lx:1:1:D:0 GNQ:-:1:V:0 ST:00:1:V:0
-WC:100:1:S:0 ST:01:1:V:0 DI:10:0:S:0 E0:03:0:V:0 O0:12:0:P:0 Lx:2:1:D:0 S1:02:1:P:0 DI:11:0:S:0
-S1:10:1:P:0 WC:101:1:S:0 ST:02:1:V:0 E0:12:0:S:0 XQ:1:0:V:0 Lx:3:1:D:0 S1:03:1:P:0 WT:110:1:P:0
-DT:00:1:P:0 WC:110:1:S:0 DC:00:1:S:0 ST:03:1:V:0 WT:111:1:P:0 WC:111:1:S:0 S1:11:1:P:0 Lz:1:1:D:0
-ST:10:1:V:0 DPQ:1:0:V:0 DI:00:1:S:0 S1:12:1:P:0 S1:13:1:P:0 XNQ:-:0:V:0 O1:10:0:P:0 ST:11:1:V:0
-O1:00:0:P:0 ST:12:1:V:0 O1:11:0:P:0 E1:10:0:S:0 E1:00:0:S:0 E1:11:0:S:0 O1:12:0:P:0 E1:12:0:S:0
-F0:00:0:D:0 ST:13:1:V:0 O1:01:0:P:0 E1:01:0:S:0 WQ:10:1:V:0 WQ:11:1:V:0 DT:01:1:P:0 DT:10:1:P:0
-DI:10:1:V:0 DI:01:1:V:0 DI:11:1:V:0 DC:01:1:S:0 DC:10:1:S:0 DT:11:1:P:0 O0:13:0:P:0 DPQ:0:1:V:0
-DN:-:1:V:0 O1:02:0:P:0 O1:03:0:P:0 O1:13:0:P:0 E1:02:0:V:0 E0:13:0:S:0 DC:11:1:S:0 DKQ:0:1:V:0
-XT:0:1:P:0 XT:1:1:P:0 DPQ:1:1:V:0 DKQ:1:1:V:0 E1:03:0:S:0 E1:13:0:S:0 F1:10:0:D:0 O0:00:1:P:0
-XC:0:1:S:0 XC:1:1:S:0 O0:01:1:P:0 XT:2:1:P:0 F1:00:0:D:0 XT:3:1:P:0 O0:10:1:P:0 XC:2:1:S:0
-F0:10:0:D:0 E0:10:1:S:0 O0:11:1:P:0 E0:00:1:V:0 E0:11:1:S:0 E0:01:1:V:0 O0:12:1:P:0 XC:3:1:V:0
-XQ:0:1:V:0 F1:12:0:D:0 O0:13:1:P:0 F1:02:0:D:0 XN:-:1:V:0 F0:00:1:D:0 F0:10:1:D:0 E0:12:1:S:0
-XQ:1:1:V:0 O0:02:1:P:0 E0:13:1:S:0 XNQ:-:1:V:0 O0:03:1:P:0 O1:00:1:P:0 E0:02:1:V:0 O1:01:1:P:0
-E0:03:1:S:0 O1:02:1:P:0 E1:00:1:S:0 O1:03:1:P:0 F0:12:1:D:0 F0:02:1:D:0 O1:10:1:P:0 E1:01:1:V:0
-F1:00:1:D:0 O1:11:1:P:0 E1:02:1:S:0 F1:01:1:D:0 E1:10:1:V:0 O1:12:1:P:0 E1:03:1:S:0 F1:02:1:D:0
-F1:03:1:D:0 E1:11:1:S:0 E1:12:1:V:0 O1:13:1:P:0 E1:13:1:S:0 F1:10:1:D:0 F1:11:1:D:0 F1:12:1:D:0
-F1:13:1:D:0
+load.g/0 load.w2/0*2 busy/0+9 load.w1/0 load.g/0 w2.turn/0 load.g/0 w2.turn/0+2 w2.pack/0/v load.g/0 g.pack/0/v
+g.pack/0/s load.w1/0 w2.turn/0+1 w2.pack/0/s w1.turn/0 w2.quant/0 load.z/0 g.pack/0/s w2.turn/0+3 w2.pack/0/v
+w1.pack/0/s g.pack/0/v g.pack/0/s g.pack/0/v*2 load.w2/1 g.quant/0 w1.turn/0+3 w1.turn/0 w2.pack/0/s g.pack/0/s
+w2.quant/0 load.z/0 w1.pack/0/s*2 g.quant/0 w1.turn/0 g.negate/0 dh0.mul/0*3 w1.pack/0/s w1.quant/0 dz0.mask/0*3
+load.w2/1 dh0.mul/0 load.x/0*2 dzk0.turn/0 dz0.mask/0 w2.turn/1*2 dzk0.pack/0/s g.quant-/0 w2.pack/1/s
+dzk0.turn/0 dzp0.pack/0/v load.x/0*2 dh1.mul/0*3 dzk0.pack/0/s w2.pack/1/s dz1.mask/0*3 dzp0.pack/0/s dh1.mul/0
+load.g/1 dzk1.turn/0 load.w1/1 dz1.mask/0 w2.turn/1*2 dzk1.pack/0/s dzk.negate/0 w2.pack/1/s*2 dzk1.turn/0+3
+load.g/1*2 w1.quant/0 dzp1.pack/0/v x.turn/0 x.turn/0+3 load.g/1 dzp.quant/0 dzk1.pack/0/s w2.quant/1 load.w1/1
+x.pack/0/s*2 dzk.quant/0*2 x.turn/0*2 g.pack/1/v*4 load.x/1 dx0.mul/0*3 x.pack/0/s*2 load.z/1 g.pack/1/v*3
+dx0.mul/0 w1.turn/1*3 dx0.copy/0/s w2.quant/1 g.pack/1/s x.negate/0 load.x/1 g.quant/1*2 dx0.copy/0/s*3
+dx1.mul/0*2 load.z/1 g.negate/1 dh0.mul/1*3 dx1.copy/0/s*2 x.quant-/0 g.quant-/1 w1.pack/1/s load.x/1
+dz0.mask/1*3 dh0.mul/1 dzp1.pack/0/s dx1.mul/0 dx0.store/0 dh1.mul/1*3 dx1.copy/0/s x.quant/0 w1.pack/1/s*2
+dz0.mask/1 dzp.quant/0 w1.turn/1 load.x/1 dzk0.turn/1*2 x.quant/0 dzp0.pack/1/s dz1.mask/1*3 dh1.mul/1 dw1.mul/0
+w1.pack/1/s dx1.mul/0 dzk0.pack/1/s w1.quant/1 dw0.mul/0 dw1.copy/0/s dz1.mask/1 dw1.mul/0 dzk0.pack/1/s
+dzp0.pack/1/v dx1.copy/0/s dzk1.turn/1*2 dw0.copy/0/s dzk.negate/1 dx1.store/0 dw1.mul/0*2 dw1.copy/0/s
+dzp.quant/1 dzk1.pack/1/s*2 dzp1.pack/1/v dw0.mul/0*2 w1.quant/1 dw1.copy/0/s*2 dw1.store/0 dzk.quant/1
+x.turn/1*2 dw0.copy/0/s dw0.copy/0/v x.pack/1/s dw0.store/0 dzk.quant/1 dx0.mul/1 dw0.mul/0 dzp1.pack/1/v
+dx0.copy/1/s dw1.store/0 dx0.mul/1 dw0.copy/0/v dx1.mul/1*2 dx0.copy/1/s dw0.store/0 x.pack/1/s dx1.copy/1/v
+x.turn/1*2 dzp.quant/1 dx0.store/1 dx1.copy/1/v x.pack/1/s dx1.mul/1*2 x.pack/1/v dx1.store/1 dx1.copy/1/s*2
+dx0.mul/1*2 x.quant/1*2 dx0.copy/1/s*2 dx1.store/1 x.negate/1 dw0.mul/1*3 dx0.store/1 x.quant-/1 dw0.copy/1/s*3
+dw0.store/1*3 dw1.mul/1*4 dw1.copy/1/s*2 dw1.store/1*2 dw1.copy/1/v dw0.mul/1 dw1.copy/1/s dw1.store/1*2
+dw0.copy/1/s dw0.store/1
 """
-T_BANKS = 3
-M_BANKS = 5
-OUT_BUFS = 8
 
 
 def tile_scatteringmodule_pa_v_kernel(tc, xh, w1, w2, b1, b2, z1, grad_out, out_0, out_1):
     nc = tc.nc
-    g_hbm = grad_out.rearrange("b (n p t) o h w r -> n p b (t o h w r)", n=NB, t=4)
-    x_hbm = xh.rearrange("b (n p t) o h w r -> n p b (t o h w r)", n=NB, t=4)
-    w_hbm = {"1": w1.rearrange("r n (p a) k -> r n p a k", a=4), "2": w2.rearrange("r n (p a) k -> r n p a k", a=4)}
-    z_hbm = z1.rearrange("r n (m t) k -> r n m t k", t=4)
-    o0_hbm = out_0.rearrange("b (n p a) o h w r -> n p b (a o h w r)", n=NB, a=4)
-    o1_hbm = out_1.rearrange("r n (p a) k -> r n p a k", a=4)
+    g_hbm = grad_out.rearrange("b (n p t) o h w r -> n b p (t o h w r)", n=NB, t=PACK)
+    x_hbm = xh.rearrange("b (n p a) o h w r -> n b p a (o h w r)", n=NB, a=4)
+    w_hbm = {
+        "w1": w1.rearrange("r n (p a) k -> n r p a k", a=4),
+        "w2": w2.rearrange("r n (p a) k -> n r p a k", a=4),
+    }
+    z_hbm = z1.rearrange("r n (p t) k -> n r p t k", t=4)
+    dx_hbm = out_0.rearrange("b (n p a) o h w r -> n p b (a o h w r)", n=NB, a=4)
+    dw_hbm = out_1.rearrange("r n (p a) k -> n r p a k", a=4)
 
     with ExitStack() as ctx:
         const = ctx.enter_context(tc.tile_pool(name="const", bufs=1))
-        raw = ctx.enter_context(tc.tile_pool(name="raw", bufs=1))
-        grp = ctx.enter_context(tc.tile_pool(name="grp", bufs=1))
-        mx = ctx.enter_context(tc.tile_pool(name="mx", bufs=1))
+        sbuf = ctx.enter_context(tc.tile_pool(name="sbuf", bufs=1))
         outs = ctx.enter_context(tc.tile_pool(name="outs", bufs=OUT_BUFS))
-        tps = ctx.enter_context(tc.psum_pool(name="tps", bufs=T_BANKS))
-        mps = ctx.enter_context(tc.psum_pool(name="mps", bufs=M_BANKS))
+        turn_psum = ctx.enter_context(tc.psum_pool(name="turn_psum", bufs=TURN_BANKS))
+        mul_psum = ctx.enter_context(tc.psum_pool(name="mul_psum", bufs=MUL_BANKS))
 
         ident = const.tile([P, P], F32, name="ident")
         make_identity(nc, ident[:])
         zeros = const.tile([P, BS], BF16, name="zeros")
         nc.gpsimd.memset(zeros[:], 0.0)
 
-        def warm(t, count):
+        made = {}
+        banks = {}
+
+        def sb(n, name):
+            if (n, name) not in made:
+                shape, dtype, bufs = TILES[name]
+                made[n, name] = sbuf.tile([P] + list(shape), dtype, name=name, tag=name, bufs=bufs, align_bytes=64)
+            return made[n, name]
+
+        def out_tile(n, key, shape, bufs):
+            if (n, key) not in made:
+                tag = "out%d" % bufs
+                made[n, key] = outs.tile(shape, F32, name=tag, tag=tag, bufs=bufs)
+            return made[n, key]
+
+        def move(engine):
+            return {"v": nc.vector.tensor_copy, "s": nc.scalar.copy}[engine]
+
+        def keep_busy(bank, count):
             for i in range(count):
-                nc.tensor.matmul(t, lhsT=zeros[:, 0:P], rhs=zeros[:], start=True, stop=True)
+                nc.tensor.matmul(bank, lhsT=zeros[:, 0:P], rhs=zeros[:], start=True, stop=True)
 
-        def HD(n, i, j, e):
-            t = mps.tile([P, BS], F32, name="mm", tag="mm")
-            warm(t[:], i)
-
-        def quant(cs, grouped, lo, hi, fmt):
+        def quantise(n, name, words, lo, hi, fmt):
             nc.vector.quantize_mx(
-                out=cs[0][:, lo:hi].bitcast(fmt), scales=cs[1][:, lo:hi], in_=grouped[:, 4 * lo : 4 * hi]
+                out=sb(n, name + "_codes")[:, lo:hi].bitcast(fmt),
+                scales=sb(n, name + "_scales")[:, lo:hi],
+                in_=words[:, PACK * lo : PACK * hi],
             )
 
-        def mm(out, l, llo, lf, r, rlo, rf, start, stop):
-            nc.tensor.matmul_mx(
-                out=out,
-                lhsT=l[0][:, llo : llo + 128].bitcast(lf),
-                lhsT_scale=l[1][:, llo : llo + 128],
-                rhs=r[0][:, rlo : rlo + 512].bitcast(rf),
-                rhs_scale=r[1][:, rlo : rlo + 512],
-                start=start,
-                stop=stop,
-            )
-
-        tiles = {}
-
-        def get(n, key, shape, dt, pool, bufs=1):
-            if (n, key) not in tiles:
-                t = pool.tile(shape, dt, name=key, tag=key, bufs=bufs, align_bytes=64)
-                tiles[n, key] = t
-            return tiles[n, key]
-
-        def codes(n, key, width, bufs=1):
-            return get(n, key + "_c", [P, width], U32, mx, bufs), get(n, key + "_s", [P, width], U8, mx, bufs)
-
-        def bank(n, key, shape, pool, tag):
-            t = pool.tile(shape, F32, name=tag, tag=tag)
-            tiles[n, key] = t
-            return t
-
-        def copy(engine):
-            return nc.vector.tensor_copy if engine == "V" else nc.scalar.copy
-
-        def g_raw(n):
-            return get(n, "g_raw", [P, 4, 4, 256], BF16, raw)
-
-        def x_raw(n):
-            return get(n, "x_raw", [P, 4, 4, 256], BF16, raw)
-
-        def w_raw(n, k, r):
-            return get(n, "w%s_raw%d" % (k, r), [P, 4, BS], BF16, raw)
-
-        def z_raw(n, r):
-            return get(n, "z_raw%d" % r, [P, 4, BS], F32, raw)
-
-        def g_grp(n):
-            return get(n, "g_grp", [P, 3, 4, P, 4], BF16, grp)
-
-        def w_grp(n, k):
-            return get(n, "w%s_grp" % k, [P, 2, 4, P, 4], BF16, grp)
-
-        def dz_tile(n, r):
-            return get(n, "dz%d" % r, [P, 4, BS], BF16, grp)
-
-        def dp_grp(n):
-            return get(n, "dp_grp", [P, 2, BS, 4], BF16, grp)
-
-        def dk_grp(n):
-            return get(n, "dk_grp", [P, 2, 3, 256, 4], BF16, grp)
-
-        def x_grp(n):
-            return get(n, "x_grp", [P, 3, 4, P, 4], BF16, grp)
-
-        def out_tile(n, key, shape, tag, bufs):
-            if (n, key) not in tiles:
-                t = outs.tile(shape, F32, name=tag, tag=tag, bufs=bufs)
-                tiles[n, key] = t
-            return tiles[n, key]
-
-        def Lg(n, b, j, e):
-            nc.sync.dma_start(out=g_raw(n)[:, b].rearrange("p t q -> p (t q)"), in_=g_hbm[n][:, b, :])
-
-        def Lx(n, b, j, e):
-            nc.sync.dma_start(out=x_raw(n)[:, :, b, :], in_=x_hbm[n][:, b, :].rearrange("p (a q) -> p a q", a=4))
-
-        def Lw1(n, r, j, e):
-            nc.sync.dma_start(out=w_raw(n, "1", r)[:], in_=w_hbm["1"][r][n])
-
-        def Lw2(n, r, j, e):
-            nc.sync.dma_start(out=w_raw(n, "2", r)[:], in_=w_hbm["2"][r][n])
-
-        def Lz(n, r, j, e):
-            nc.sync.dma_start(out=z_raw(n, r)[:], in_=z_hbm[r][n])
-
-        def GC(n, b, ri, e):
-            src = g_raw(n)[:, b].rearrange("p t (m j r) -> p r m j t", j=4, r=2)[:, ri]
-            dst = g_grp(n)[:, ri, :, 32 * b : 32 * b + 32, :].rearrange("p j m t -> p m j t")
-            copy(e)(out=dst, in_=src)
-
-        def GQ(n, ri, j, e):
-            quant(codes(n, "g", 1536), g_grp(n)[:].rearrange("p s j m t -> p (s j m t)"), 512 * ri, 512 * ri + 512, E5)
-
-        def GN(n, i, j, e):
-            gg = g_grp(n)[:].rearrange("p s j m t -> p s (j m t)")
-            nc.vector.tensor_scalar_mul(out=gg[:, 2], in0=gg[:, 0], scalar1=-1.0)
-
-        def GNQ(n, i, j, e):
-            quant(codes(n, "g", 1536), g_grp(n)[:].rearrange("p s j m t -> p (s j m t)"), 1024, 1536, E5)
-
-        def WT(n, k, r, half, d):
-            words = w_raw(n, k, r)[:].rearrange("p a k -> p (a k)").bitcast(F32)
-            t = bank(n, "wt%s%d%d" % (k, r, half), [P, 2, 2, P], tps, "tp")
-            warm(t[:].rearrange("p a u m -> p (a u m)"), d)
-            for a in range(2):
-                for u in range(2):
-                    lo = (2 * half + a) * 256 + u
-                    nc.tensor.transpose(t[:, a, u, :], words[:, lo : lo + 255 : 2], ident[:])
-
-        def WC(n, k, r, half, e):
-            t = tiles[n, "wt%s%d%d" % (k, r, half)]
-            dst = w_grp(n, k)[:, r, 2 * half : 2 * half + 2].rearrange("p a m t -> p (a m t)").bitcast(F32)
-            copy(e)(out=dst.rearrange("p (a m u) -> p a m u", a=2, u=2), in_=t[:].rearrange("p a u m -> p a m u"))
-
-        def WQ(n, k, r):
-            quant(
-                codes(n, "w" + k, 1024, 2 if k == "1" else 1),
-                w_grp(n, k)[:].rearrange("p r a m t -> p (r a m t)"),
-                512 * r,
-                512 * r + 512,
-                E4,
-            )
-
-        def S1(n, r, j, e):
-            t = bank(n, "s1%d%d" % (r, j), [P, BS], mps, "mm")
-            gc, wc = codes(n, "g", 1536), codes(n, "w2", 1024)
-            pairs = ((0, 0), (512, 512)) if r == 0 else ((512, 0), (1024, 512))
-            for i, (glo, wlo) in enumerate(pairs):
-                mm(t[:], gc, glo + 128 * j, E5, wc, wlo, E4, i == 0, i == 1)
-
-        def ST(n, r, j, e):
-            t = tiles[n, "s1%d%d" % (r, j)]
-            z = z_raw(n, r)[:, j].rearrange("p (k u e) -> p u k e", u=2, e=2)
-            dz = dz_tile(n, r)[:, j].rearrange("p (u k e) -> p u k e", u=2, e=2)
-            b4 = t[:].rearrange("p (u e k) -> p u k e", u=2, e=2)
-            for u in range(2):
-                nc.vector.scalar_tensor_tensor(
-                    out=dz[:, u], in0=z[:, u], scalar=0.0, in1=b4[:, u], op0=ALU.is_gt, op1=ALU.mult
+        def multiply(n, bank, left, left_fmt, right, right_fmt, columns):
+            for i, (lo, ro) in enumerate(columns):
+                nc.tensor.matmul_mx(
+                    out=bank,
+                    lhsT=sb(n, left + "_codes")[:, lo : lo + P].bitcast(left_fmt),
+                    lhsT_scale=sb(n, left + "_scales")[:, lo : lo + P],
+                    rhs=sb(n, right + "_codes")[:, ro : ro + BS].bitcast(right_fmt),
+                    rhs_scale=sb(n, right + "_scales")[:, ro : ro + BS],
+                    start=(i == 0),
+                    stop=(i == len(columns) - 1),
                 )
 
-        def DI(n, r, hf, e):
-            k = slice(256 * hf, 256 * hf + 256)
-            copy(e)(out=dp_grp(n)[:, r, k, :], in_=dz_tile(n, r)[:, :, k].rearrange("p t k -> p k t"))
+        def load_g(n, i, engine, idle):
+            nc.sync.dma_start(out=sb(n, "g_raw")[:, i].rearrange("p t q -> p (t q)"), in_=g_hbm[n][i])
 
-        def DPQ(n, r, j, e):
-            quant(codes(n, "dp", 1024, 2), dp_grp(n)[:].rearrange("p r k t -> p (r k t)"), 512 * r, 512 * r + 512, E5)
+        def load_x(n, i, engine, idle):
+            nc.sync.dma_start(out=sb(n, "x_raw")[:, :, i, :], in_=x_hbm[n][i])
 
-        def DT(n, r, u, e):
-            words = dz_tile(n, r)[:].rearrange("p t k -> p (t k)").bitcast(F32)
-            t = bank(n, "dt%d%d" % (r, u), [P, 2, 2, P], tps, "tp")
-            warm(t[:].rearrange("p a u m -> p (a u m)"), e)
-            for i in range(2):
-                for v in range(2):
-                    lo = (2 * u + i) * 256 + v * 128
-                    nc.tensor.transpose(t[:, i, v, :], words[:, lo : lo + 128], ident[:])
+        def load_w(which):
+            def step(n, i, engine, idle):
+                nc.sync.dma_start(out=sb(n, "%s_raw%d" % (which, i))[:], in_=w_hbm[which][n][i])
 
-        def DC(n, r, u, e):
-            t = tiles[n, "dt%d%d" % (r, u)]
-            dst = dk_grp(n)[:].rearrange("p h s q t -> p (h s q t)").bitcast(F32)
-            dst = dst.rearrange("p (h s m x) -> p s h m x", h=2, s=3, x=8)[:, r]
-            dst = dst[:, :, :, 4 * u : 4 * u + 4].rearrange("p h m (e v) -> p h m e v", e=2)
-            copy(e)(out=dst, in_=t[:].rearrange("p e v (h m) -> p h m e v", h=2))
+            return step
 
-        def DN(n, i, j, e):
-            d = dk_grp(n)[:].rearrange("p h s q t -> p s h (q t)")
-            nc.vector.tensor_scalar_mul(out=d[:, 2], in0=d[:, 0], scalar1=-1.0)
+        def load_z(n, i, engine, idle):
+            nc.sync.dma_start(out=sb(n, "z_raw%d" % i)[:], in_=z_hbm[n][i])
 
-        def DKQ(n, h, j, e):
-            d = dk_grp(n)[:].rearrange("p h s q t -> p (h s q t)")
-            cs = codes(n, "dk", 1536, 2)
-            quant(cs, d, 768 * h, 768 * h + 512, E5)
-            quant(cs, d, 768 * h + 512, 768 * h + 768, E5)
+        def g_pack(n, i, engine, idle):
+            b, part = divmod(i, 2)
+            src = sb(n, "g_raw")[:, b].rearrange("p t (m j r) -> p r m j t", j=4, r=2)[:, part]
+            dst = sb(n, "g_words")[:, part, :, 32 * b : 32 * b + 32, :].rearrange("p j m t -> p m j t")
+            move(engine)(out=dst, in_=src)
 
-        def XT(n, a, j, e):
-            t = bank(n, "xt%d" % a, [P, 4, P], tps, "tp")
-            warm(t[:].rearrange("p t c -> p (t c)"), e)
-            words = x_raw(n)[:].rearrange("p a b q -> p (a b q)").bitcast(F32)
-            for i in range(4):
-                nc.tensor.transpose(t[:, i, :], words[:, 512 * a + i : 512 * a + 512 : 4], ident[:])
+        def g_words(n):
+            return sb(n, "g_words")[:].rearrange("p s j m t -> p (s j m t)")
 
-        def XC(n, a, j, e):
-            t = tiles[n, "xt%d" % a]
-            src = t[:].rearrange("p t c -> p (t c)").bitcast(BF16).rearrange("p (t c r) -> p r c t", t=4, r=2)
-            copy(e)(out=x_grp(n)[:, 0:2, a], in_=src)
+        def g_quant(n, i, engine, idle):
+            quantise(n, "g", g_words(n), BS * i, BS * (i + 1), E5M2)
 
-        def XQ(n, ri, j, e):
-            quant(codes(n, "x", 1536, 2), x_grp(n)[:].rearrange("p s a m t -> p (s a m t)"), 512 * ri, 512 * ri + 512, E4)
+        def g_negate(n, i, engine, idle):
+            g = sb(n, "g_words")[:].rearrange("p s j m t -> p s (j m t)")
+            nc.vector.tensor_scalar_mul(out=g[:, NEG], in0=g[:, RE], scalar1=-1.0)
 
-        def XN(n, i, j, e):
-            g = x_grp(n)[:].rearrange("p s a m t -> p s (a m t)")
-            nc.vector.tensor_scalar_mul(out=g[:, 2], in0=g[:, 1], scalar1=-1.0)
+        def g_quant_negative(n, i, engine, idle):
+            quantise(n, "g", g_words(n), BS * NEG, BS * (NEG + 1), E5M2)
 
-        def XNQ(n, i, j, e):
-            quant(codes(n, "x", 1536, 2), x_grp(n)[:].rearrange("p s a m t -> p (s a m t)"), 1024, 1536, E4)
+        def w_turn(which):
+            def step(n, i, engine, idle):
+                part, half = divmod(i, 2)
+                words = sb(n, "%s_raw%d" % (which, part))[:].rearrange("p a k -> p (a k)").bitcast(F32)
+                bank = turn_psum.tile([P, 2, 2, P], F32, name="turn", tag="turn")
+                keep_busy(bank[:].rearrange("p a u m -> p (a u m)"), idle)
+                for a in range(2):
+                    for u in range(2):
+                        lo = ROW * (2 * half + a) + u
+                        nc.tensor.transpose(bank[:, a, u, :], words[:, lo : lo + ROW - 1 : 2], ident[:])
+                banks[n, which, i] = bank
 
-        def O1(n, r, a, e):
-            t = bank(n, "o1%d%d" % (r, a), [P, BS], mps, "mm")
-            xc, dc = codes(n, "x", 1536, 2), codes(n, "dp", 1024, 2)
-            pairs = ((0, 0), (512, 512)) if r == 0 else ((0, 512), (1024, 0))
-            for i, (xlo, dlo) in enumerate(pairs):
-                mm(t[:], xc, xlo + 128 * a, E4, dc, dlo, E5, i == 0, i == 1)
+            return step
 
-        def E1(n, r, a, e):
-            t = tiles[n, "o1%d%d" % (r, a)]
-            o = out_tile(n, "O1%d%d" % (r, a // 2), [P, 2, BS], "o2", OUT_BUFS)
-            copy(e)(
-                out=o[:, a % 2].rearrange("p (k u e) -> p k u e", u=2, e=2),
-                in_=t[:].rearrange("p (u k e) -> p k u e", u=2, e=2),
+        def w_pack(which):
+            def step(n, i, engine, idle):
+                part, half = divmod(i, 2)
+                dst = sb(n, which + "_words")[:, part, 2 * half : 2 * half + 2]
+                dst = dst.rearrange("p a m t -> p (a m t)").bitcast(F32)
+                move(engine)(
+                    out=dst.rearrange("p (a m u) -> p a m u", a=2, u=2),
+                    in_=banks[n, which, i][:].rearrange("p a u m -> p a m u"),
+                )
+
+            return step
+
+        def w_quant(which):
+            def step(n, i, engine, idle):
+                words = sb(n, which + "_words")[:].rearrange("p r a m t -> p (r a m t)")
+                quantise(n, which, words, BS * i, BS * (i + 1), E4M3)
+
+            return step
+
+        def dh_mul(part):
+            terms = ((RE, RE), (IM, IM)) if part == RE else ((IM, RE), (NEG, IM))
+
+            def step(n, i, engine, idle):
+                bank = mul_psum.tile([P, BS], F32, name="mul", tag="mul")
+                columns = [(BS * g + P * i, BS * w) for g, w in terms]
+                multiply(n, bank[:], "g", E5M2, "w2", E4M3, columns)
+                banks[n, "dh%d" % part, i] = bank
+
+            return step
+
+        def dz_mask(part):
+            def step(n, i, engine, idle):
+                z = sb(n, "z_raw%d" % part)[:, i].rearrange("p (c u e) -> p u c e", u=2, e=2)
+                dh = banks[n, "dh%d" % part, i][:].rearrange("p (u e c) -> p u c e", u=2, e=2)
+                dz = sb(n, "dz%d" % part)[:, i].rearrange("p (u c e) -> p u c e", u=2, e=2)
+                for u in range(2):
+                    nc.vector.scalar_tensor_tensor(
+                        out=dz[:, u], in0=z[:, u], scalar=0.0, in1=dh[:, u], op0=ALU.is_gt, op1=ALU.mult
+                    )
+
+            return step
+
+        def dzp_pack(part):
+            def step(n, i, engine, idle):
+                k = slice(ROW * i, ROW * (i + 1))
+                src = sb(n, "dz%d" % part)[:, :, k].rearrange("p t k -> p k t")
+                move(engine)(out=sb(n, "dzp_words")[:, part, k, :], in_=src)
+
+            return step
+
+        def dzp_quant(n, i, engine, idle):
+            words = sb(n, "dzp_words")[:].rearrange("p r k t -> p (r k t)")
+            quantise(n, "dzp", words, BS * i, BS * (i + 1), E5M2)
+
+        def dzk_turn(part):
+            def step(n, i, engine, idle):
+                words = sb(n, "dz%d" % part)[:].rearrange("p t k -> p (t k)").bitcast(F32)
+                bank = turn_psum.tile([P, 2, 2, P], F32, name="turn", tag="turn")
+                keep_busy(bank[:].rearrange("p e u m -> p (e u m)"), idle)
+                for e in range(2):
+                    for u in range(2):
+                        lo = ROW * (2 * i + e) + P * u
+                        nc.tensor.transpose(bank[:, e, u, :], words[:, lo : lo + P], ident[:])
+                banks[n, "dzk%d" % part, i] = bank
+
+            return step
+
+        def dzk_pack(part):
+            def step(n, i, engine, idle):
+                dst = sb(n, "dzk_words")[:].rearrange("p h s q t -> p (h s q t)").bitcast(F32)
+                dst = dst.rearrange("p (h s m x) -> p s h m x", h=2, s=3, x=8)[:, part]
+                dst = dst[:, :, :, 4 * i : 4 * i + 4].rearrange("p h m (e u) -> p h m e u", e=2)
+                src = banks[n, "dzk%d" % part, i][:].rearrange("p e u (h m) -> p h m e u", h=2)
+                move(engine)(out=dst, in_=src)
+
+            return step
+
+        def dzk_negate(n, i, engine, idle):
+            d = sb(n, "dzk_words")[:].rearrange("p h s q t -> p s h (q t)")
+            nc.vector.tensor_scalar_mul(out=d[:, NEG], in0=d[:, RE], scalar1=-1.0)
+
+        def dzk_quant(n, i, engine, idle):
+            words = sb(n, "dzk_words")[:].rearrange("p h s q t -> p (h s q t)")
+            lo = 3 * ROW * i
+            quantise(n, "dzk", words, lo, lo + 2 * ROW, E5M2)
+            quantise(n, "dzk", words, lo + 2 * ROW, lo + 3 * ROW, E5M2)
+
+        def x_turn(n, i, engine, idle):
+            words = sb(n, "x_raw")[:].rearrange("p a b q -> p (a b q)").bitcast(F32)
+            bank = turn_psum.tile([P, 4, P], F32, name="turn", tag="turn")
+            keep_busy(bank[:].rearrange("p t m -> p (t m)"), idle)
+            for t in range(4):
+                lo = BS * i
+                nc.tensor.transpose(bank[:, t, :], words[:, lo + t : lo + BS : 4], ident[:])
+            banks[n, "x", i] = bank
+
+        def x_pack(n, i, engine, idle):
+            src = banks[n, "x", i][:].rearrange("p t m -> p (t m)").bitcast(BF16)
+            move(engine)(
+                out=sb(n, "x_words")[:, RE : IM + 1, i], in_=src.rearrange("p (t m r) -> p r m t", t=4, r=2)
             )
 
-        def F1(n, r, a, e):
-            w = 2 - n
-            nc.sync.dma_start(
-                out=o1_hbm[r][n][:, a : a + w], in_=tiles[n, "O1%d%d" % (r, a // 2)][:, a % 2 : a % 2 + w]
-            )
+        def x_words(n):
+            return sb(n, "x_words")[:].rearrange("p s a m t -> p (s a m t)")
 
-        def O0(n, h, a, e):
-            t = bank(n, "o0%d%d" % (h, a), [P, BS], mps, "mm")
-            wc, dc = codes(n, "w1", 1024, 2), codes(n, "dk", 1536, 2)
-            mm(t[:], wc, 128 * a, E4, dc, 768 * h, E5, True, False)
-            mm(t[:], wc, 512 + 128 * a, E4, dc, 768 * h + 256, E5, False, True)
+        def x_quant(n, i, engine, idle):
+            quantise(n, "x", x_words(n), BS * i, BS * (i + 1), E4M3)
 
-        def E0(n, h, a, e):
-            t = tiles[n, "o0%d%d" % (h, a)]
-            w = 4 - 2 * n
-            o = out_tile(n, "O0%d%d" % (h, a // w), [P, 2, w, 256], "o%d" % w, 2 if w == 4 else OUT_BUFS)
-            copy(e)(
-                out=o[:, :, a % w].rearrange("p b (q r) -> p b q r", r=2),
-                in_=t[:].rearrange("p (r b q) -> p b q r", r=2, b=2),
-            )
+        def x_negate(n, i, engine, idle):
+            x = sb(n, "x_words")[:].rearrange("p s a m t -> p s (a m t)")
+            nc.vector.tensor_scalar_mul(out=x[:, NEG], in0=x[:, IM], scalar1=-1.0)
 
-        def F0(n, h, a, e):
-            w = 4 - 2 * n
-            nc.sync.dma_start(
-                out=o0_hbm[n][:, 2 * h : 2 * h + 2, 256 * a : 256 * (a + w)],
-                in_=tiles[n, "O0%d%d" % (h, a // w)][:].rearrange("p b a q -> p b (a q)"),
-            )
+        def x_quant_negative(n, i, engine, idle):
+            quantise(n, "x", x_words(n), BS * NEG, BS * (NEG + 1), E4M3)
 
-        plain = {
-            "HD": HD, "Lg": Lg, "Lx": Lx, "Lw1": Lw1, "Lw2": Lw2, "Lz": Lz, "GC": GC, "GQ": GQ, "GN": GN, "GNQ": GNQ,
-            "S1": S1, "ST": ST, "DI": DI, "DPQ": DPQ, "DT": DT, "DC": DC, "DN": DN, "DKQ": DKQ, "XT": XT,
-            "XC": XC, "XQ": XQ, "XN": XN, "XNQ": XNQ, "O1": O1, "E1": E1, "F1": F1, "O0": O0, "E0": E0, "F0": F0,
+        def dw_mul(part):
+            terms = ((RE, RE), (IM, IM)) if part == RE else ((RE, IM), (NEG, RE))
+
+            def step(n, i, engine, idle):
+                bank = mul_psum.tile([P, BS], F32, name="mul", tag="mul")
+                columns = [(BS * x + P * i, BS * d) for x, d in terms]
+                multiply(n, bank[:], "x", E4M3, "dzp", E5M2, columns)
+                banks[n, "dw%d" % part, i] = bank
+
+            return step
+
+        def dw_copy(part):
+            def step(n, i, engine, idle):
+                out = out_tile(n, "dw%d_%d" % (part, i // 2), [P, 2, BS], OUT_BUFS)
+                move(engine)(
+                    out=out[:, i % 2].rearrange("p (c u e) -> p c u e", u=2, e=2),
+                    in_=banks[n, "dw%d" % part, i][:].rearrange("p (u c e) -> p c u e", u=2, e=2),
+                )
+
+            return step
+
+        def dw_store(part):
+            def step(n, i, engine, idle):
+                wide = 2 - n
+                a = wide * i
+                out = made[n, "dw%d_%d" % (part, a // 2)]
+                nc.sync.dma_start(out=dw_hbm[n][part][:, a : a + wide], in_=out[:, a % 2 : a % 2 + wide])
+
+            return step
+
+        def dx_mul(half):
+            def step(n, i, engine, idle):
+                bank = mul_psum.tile([P, BS], F32, name="mul", tag="mul")
+                lo = 3 * ROW * half
+                columns = [(P * i, lo), (BS + P * i, lo + ROW)]
+                multiply(n, bank[:], "w1", E4M3, "dzk", E5M2, columns)
+                banks[n, "dx%d" % half, i] = bank
+
+            return step
+
+        def dx_wide(n):
+            return 4 - 2 * n
+
+        def dx_copy(half):
+            def step(n, i, engine, idle):
+                wide = dx_wide(n)
+                bufs = 2 if n == 0 else OUT_BUFS
+                out = out_tile(n, "dx%d_%d" % (half, i // wide), [P, 2, wide, ROW], bufs)
+                move(engine)(
+                    out=out[:, :, i % wide].rearrange("p b (q r) -> p b q r", r=2),
+                    in_=banks[n, "dx%d" % half, i][:].rearrange("p (r b q) -> p b q r", r=2, b=2),
+                )
+
+            return step
+
+        def dx_store(half):
+            def step(n, i, engine, idle):
+                wide = dx_wide(n)
+                a = wide * i
+                nc.sync.dma_start(
+                    out=dx_hbm[n][:, 2 * half : 2 * half + 2, ROW * a : ROW * (a + wide)],
+                    in_=made[n, "dx%d_%d" % (half, i)][:].rearrange("p b a q -> p b (a q)"),
+                )
+
+            return step
+
+        def busy(n, i, engine, idle):
+            bank = mul_psum.tile([P, BS], F32, name="mul", tag="mul")
+            keep_busy(bank[:], idle)
+
+        steps = {
+            "load.g": load_g,
+            "load.x": load_x,
+            "load.z": load_z,
+            "g.pack": g_pack,
+            "g.quant": g_quant,
+            "g.negate": g_negate,
+            "g.quant-": g_quant_negative,
+            "dzp.quant": dzp_quant,
+            "dzk.negate": dzk_negate,
+            "dzk.quant": dzk_quant,
+            "x.turn": x_turn,
+            "x.pack": x_pack,
+            "x.quant": x_quant,
+            "x.negate": x_negate,
+            "x.quant-": x_quant_negative,
+            "busy": busy,
         }
+        for which in ("w1", "w2"):
+            steps["load." + which] = load_w(which)
+            steps[which + ".turn"] = w_turn(which)
+            steps[which + ".pack"] = w_pack(which)
+            steps[which + ".quant"] = w_quant(which)
+        for part in (RE, IM):
+            steps["dh%d.mul" % part] = dh_mul(part)
+            steps["dz%d.mask" % part] = dz_mask(part)
+            steps["dzp%d.pack" % part] = dzp_pack(part)
+            steps["dzk%d.turn" % part] = dzk_turn(part)
+            steps["dzk%d.pack" % part] = dzk_pack(part)
+            steps["dw%d.mul" % part] = dw_mul(part)
+            steps["dw%d.copy" % part] = dw_copy(part)
+            steps["dw%d.store" % part] = dw_store(part)
+        for half in range(2):
+            steps["dx%d.mul" % half] = dx_mul(half)
+            steps["dx%d.copy" % half] = dx_copy(half)
+            steps["dx%d.store" % half] = dx_store(half)
+
         ctx.enter_context(tc.manual_schedule())
-        for step in ORDER.split():
-            name, idx, n, e, d = step.split(":")
-            n = int(n)
-            d = int(d)
-            ids = [int(c) for c in idx if c != "-"]
-            if name == "HD":
-                HD(n, d, 0, e)
-            elif name == "WT":
-                WT(n, idx[0], ids[1], ids[2], d)
-            elif name == "WC":
-                WC(n, idx[0], ids[1], ids[2], e)
-            elif name == "WQ":
-                WQ(n, idx[0], ids[1])
-            else:
-                ids = ids + [0, 0]
-                plain[name](n, ids[0], ids[1], d if e == "P" else e)
+        taken = {}
+        for token in ORDER.split():
+            token, idle = token.split("+") if "+" in token else (token, "0")
+            token, count = token.split("*") if "*" in token else (token, "1")
+            kind, block, engine = (token + "/").split("/")[0:3]
+            n = int(block)
+            for repeat in range(int(count)):
+                i = taken.setdefault((kind, n), 0)
+                taken[kind, n] = i + 1
+                steps[kind](n, i, engine, int(idle))

@@ -58,28 +58,26 @@ TILES = {
 }
 
 ORDER = """
-load.g/0 load.w2/0*2 busy/0+9 load.w1/0 load.g/0 w2.turn/0 load.g/0 w2.turn/0+2 w2.pack/0/v load.g/0 g.pack/0/v
-g.pack/0/s load.w1/0 w2.turn/0+1 w2.pack/0/s w1.turn/0 w2.quant/0 load.z/0 g.pack/0/s w2.turn/0+3 w2.pack/0/v
-w1.pack/0/s g.pack/0/v g.pack/0/s g.pack/0/v*2 load.w2/1 g.quant/0 w1.turn/0+3 w1.turn/0 w2.pack/0/s g.pack/0/s
-w2.quant/0 load.z/0 w1.pack/0/s*2 g.quant/0 w1.turn/0 g.negate/0 dh0.mul/0*3 w1.pack/0/s w1.quant/0 dz0.mask/0*3
-load.w2/1 dh0.mul/0 load.x/0*2 dzk0.turn/0 dz0.mask/0 w2.turn/1*2 dzk0.pack/0/s g.quant-/0 w2.pack/1/s
-dzk0.turn/0 dzp0.pack/0/v load.x/0*2 dh1.mul/0*3 dzk0.pack/0/s w2.pack/1/s dz1.mask/0*3 dzp0.pack/0/s dh1.mul/0
-load.g/1 dzk1.turn/0 load.w1/1 dz1.mask/0 w2.turn/1*2 dzk1.pack/0/s dzk.negate/0 w2.pack/1/s*2 dzk1.turn/0+3
-load.g/1*2 w1.quant/0 dzp1.pack/0/v x.turn/0 x.turn/0+3 load.g/1 dzp.quant/0 dzk1.pack/0/s w2.quant/1 load.w1/1
-x.pack/0/s*2 dzk.quant/0*2 x.turn/0*2 g.pack/1/v*4 load.x/1 dx0.mul/0*3 x.pack/0/s*2 load.z/1 g.pack/1/v*3
-dx0.mul/0 w1.turn/1*3 dx0.copy/0/s w2.quant/1 g.pack/1/s x.negate/0 load.x/1 g.quant/1*2 dx0.copy/0/s*3
-dx1.mul/0*2 load.z/1 g.negate/1 dh0.mul/1*3 dx1.copy/0/s*2 x.quant-/0 g.quant-/1 w1.pack/1/s load.x/1
-dz0.mask/1*3 dh0.mul/1 dzp1.pack/0/s dx1.mul/0 dx0.store/0 dh1.mul/1*3 dx1.copy/0/s x.quant/0 w1.pack/1/s*2
-dz0.mask/1 dzp.quant/0 w1.turn/1 load.x/1 dzk0.turn/1*2 x.quant/0 dzp0.pack/1/s dz1.mask/1*3 dh1.mul/1 dw1.mul/0
-w1.pack/1/s dx1.mul/0 dzk0.pack/1/s w1.quant/1 dw0.mul/0 dw1.copy/0/s dz1.mask/1 dw1.mul/0 dzk0.pack/1/s
-dzp0.pack/1/v dx1.copy/0/s dzk1.turn/1*2 dw0.copy/0/s dzk.negate/1 dx1.store/0 dw1.mul/0*2 dw1.copy/0/s
-dzp.quant/1 dzk1.pack/1/s*2 dzp1.pack/1/v dw0.mul/0*2 w1.quant/1 dw1.copy/0/s*2 dw1.store/0 dzk.quant/1
-x.turn/1*2 dw0.copy/0/s dw0.copy/0/v x.pack/1/s dw0.store/0 dzk.quant/1 dx0.mul/1 dw0.mul/0 dzp1.pack/1/v
-dx0.copy/1/s dw1.store/0 dx0.mul/1 dw0.copy/0/v dx1.mul/1*2 dx0.copy/1/s dw0.store/0 x.pack/1/s dx1.copy/1/v
-x.turn/1*2 dzp.quant/1 dx0.store/1 dx1.copy/1/v x.pack/1/s dx1.mul/1*2 x.pack/1/v dx1.store/1 dx1.copy/1/s*2
-dx0.mul/1*2 x.quant/1*2 dx0.copy/1/s*2 dx1.store/1 x.negate/1 dw0.mul/1*3 dx0.store/1 x.quant-/1 dw0.copy/1/s*3
-dw0.store/1*3 dw1.mul/1*4 dw1.copy/1/s*2 dw1.store/1*2 dw1.copy/1/v dw0.mul/1 dw1.copy/1/s dw1.store/1*2
-dw0.copy/1/s dw0.store/1
+load.w2/0 load.g/0*2 busy/0+3 load.w2/0 w2.turn/0+1 w2.turn/0+2 load.g/0*2 g.pack/0/v*2 load.w1/0*2 w2.pack/0/v
+w2.pack/0/s w2.turn/0+2 w2.turn/0+3 w2.quant/0 g.pack/0/s load.z/0 g.pack/0/v w2.pack/0/s*2 g.quant/0
+w1.turn/0*3 w1.pack/0/s*3 w2.quant/0 load.g/1*2 g.negate/0 dh0.mul/0 load.w2/1 g.quant-/0 w1.turn/0 dz0.mask/0
+load.z/0 dh0.mul/0*3 w1.pack/0/s g.pack/1/s dz0.mask/0*3 dh1.mul/0 load.x/0*2 g.pack/1/s dzk0.turn/0*2
+w1.quant/0 dh1.mul/0*2 load.w2/1 dzk0.pack/0/s dzp0.pack/0/v dzp0.pack/0/s w2.turn/1*2 dz1.mask/0*3 load.x/0*2
+dzk0.pack/0/s dh1.mul/0 w2.pack/1/s*2 dzk1.turn/0+1 load.g/1*2 dz1.mask/0 dzp.quant/0 dzk1.pack/0/s dzk1.turn/0
+w2.turn/1 w2.turn/1+2 load.z/1 dzk.negate/0 dzk1.pack/0/s dzp1.pack/0/v w2.pack/1/s*2 dzk.quant/0*2 x.turn/0*3
+load.w1/1*2 x.pack/0/s*2 g.pack/1/v*2 dx0.mul/0*3 w2.quant/1 dx0.copy/0/s*2 dx1.mul/0 dx0.mul/0 g.quant/1
+dx1.copy/0/s x.turn/0 dx0.copy/0/s*2 w1.turn/1 load.x/1 dzp1.pack/0/v dh0.mul/1*3 x.pack/0/s*2 load.z/1
+g.negate/1 dzp.quant/0 dz0.mask/1*2 dx1.mul/0 dh0.mul/1 dx1.copy/0/s load.x/1*2 dx1.mul/0 g.quant-/1 w1.pack/1/s
+w1.turn/1*2 dz0.mask/1*2 w1.pack/1/s*2 load.x/1 dh1.mul/1*3 x.quant/0 dx0.store/0 dx1.copy/0/s x.negate/0
+w1.turn/1 dzp0.pack/1/v dzk0.turn/1*2 w1.pack/1/s dz1.mask/1*3 dx1.mul/0 dzk0.pack/1/s*2 dw0.mul/0*2
+dx1.copy/0/s x.quant-/0 dh1.mul/1 dw0.copy/0/s*2 w1.quant/1 dw1.mul/0*3 dw1.copy/0/s*3 dz1.mask/1 dw0.store/0
+dzp0.pack/1/v dzk1.turn/1*2 dx1.store/0 dzk.negate/1 x.turn/1 dzk1.pack/1/s*2 dzp1.pack/1/v dw0.mul/0*2
+x.pack/1/v dw0.copy/0/s*2 dw1.mul/0 dw1.store/0 dzk.quant/1*2 x.turn/1*2 dw1.copy/0/s x.pack/1/s*2 dw0.store/0
+dx0.mul/1*2 dzp1.pack/1/v dw1.store/0 dx1.mul/1*2 dx0.copy/1/v*2 x.turn/1 dzp.quant/1 dx0.store/1 dx1.copy/1/v
+dx1.copy/1/s dx1.mul/1*2 x.pack/1/s dzp.quant/1 dx1.store/1 dx0.mul/1*2 dx1.copy/1/v dx1.copy/1/s x.quant/1
+dx0.copy/1/s*2 dx1.store/1 x.negate/1 dw0.mul/1*3 dx0.store/1 x.quant-/1 dw0.copy/1/s dw0.copy/1/v dw0.store/1*2
+dw1.mul/1*3 dw0.copy/1/s dw1.copy/1/v*3 dw0.store/1 dw1.mul/1 dw1.store/1*3 dw0.mul/1 dw1.copy/1/v dw0.copy/1/s
+dw1.store/1 dw0.store/1
 """
 
 
@@ -164,16 +162,15 @@ def tile_scatteringmodule_pa_v_kernel(tc, xh, w1, w2, b1, b2, z1, grad_out, out_
             nc.sync.dma_start(out=sb(n, "z_raw%d" % i)[:], in_=z_hbm[n][i])
 
         def g_pack(n, i, engine, idle):
-            b, part = divmod(i, 2)
-            src = sb(n, "g_raw")[:, b].rearrange("p t (m j r) -> p r m j t", j=4, r=2)[:, part]
-            dst = sb(n, "g_words")[:, part, :, 32 * b : 32 * b + 32, :].rearrange("p j m t -> p m j t")
-            move(engine)(out=dst, in_=src)
+            src = sb(n, "g_raw")[:, i].rearrange("p t (m j r) -> p r m j t", j=4, r=2)
+            dst = sb(n, "g_words")[:, RE : IM + 1, :, 32 * i : 32 * i + 32, :]
+            move(engine)(out=dst.rearrange("p r j m t -> p r m j t"), in_=src)
 
         def g_words(n):
             return sb(n, "g_words")[:].rearrange("p s j m t -> p (s j m t)")
 
         def g_quant(n, i, engine, idle):
-            quantise(n, "g", g_words(n), BS * i, BS * (i + 1), E5M2)
+            quantise(n, "g", g_words(n), 0, BS * NEG, E5M2)
 
         def g_negate(n, i, engine, idle):
             g = sb(n, "g_words")[:].rearrange("p s j m t -> p s (j m t)")
@@ -211,7 +208,8 @@ def tile_scatteringmodule_pa_v_kernel(tc, xh, w1, w2, b1, b2, z1, grad_out, out_
         def w_quant(which):
             def step(n, i, engine, idle):
                 words = sb(n, which + "_words")[:].rearrange("p r a m t -> p (r a m t)")
-                quantise(n, which, words, BS * i, BS * (i + 1), E4M3)
+                parts = (i,) if which == "w2" and n == 0 else (RE, IM)
+                quantise(n, which, words, BS * parts[0], BS * (parts[-1] + 1), E4M3)
 
             return step
 
@@ -279,9 +277,8 @@ def tile_scatteringmodule_pa_v_kernel(tc, xh, w1, w2, b1, b2, z1, grad_out, out_
 
         def dzk_quant(n, i, engine, idle):
             words = sb(n, "dzk_words")[:].rearrange("p h s q t -> p (h s q t)")
-            lo = 3 * ROW * i
-            quantise(n, "dzk", words, lo, lo + 2 * ROW, E5M2)
-            quantise(n, "dzk", words, lo + 2 * ROW, lo + 3 * ROW, E5M2)
+            lo, hi = ((0, 4 * ROW), (4 * ROW, 6 * ROW))[i]
+            quantise(n, "dzk", words, lo, hi, E5M2)
 
         def x_turn(n, i, engine, idle):
             words = sb(n, "x_raw")[:].rearrange("p a b q -> p (a b q)").bitcast(F32)
@@ -302,7 +299,7 @@ def tile_scatteringmodule_pa_v_kernel(tc, xh, w1, w2, b1, b2, z1, grad_out, out_
             return sb(n, "x_words")[:].rearrange("p s a m t -> p (s a m t)")
 
         def x_quant(n, i, engine, idle):
-            quantise(n, "x", x_words(n), BS * i, BS * (i + 1), E4M3)
+            quantise(n, "x", x_words(n), 0, BS * NEG, E4M3)
 
         def x_negate(n, i, engine, idle):
             x = sb(n, "x_words")[:].rearrange("p s a m t -> p s (a m t)")

from contextlib import ExitStack

import concourse.mybir as mybir
from concourse.masks import make_identity

F32 = mybir.dt.float32
BF16 = mybir.dt.bfloat16
U32 = mybir.dt.uint32
U8 = mybir.dt.uint8
E4M3 = mybir.dt.float8_e4m3fn_x4
E5M2 = mybir.dt.float8_e5m2_x4
ALU = mybir.AluOpType

P = 128
NB = 2
BS = 512
BATCH = 4
ROW = 256
PACK = 4
FLOPS = 12 * NB * 2 * BS * BS * BS
BYTES = 2 * (4 * NB * 2 * BS * BS) + 4 * (3 * NB * 2 * BS * BS)

RE, IM, NEG = 0, 1, 2

TURN_BANKS = 3
MUL_BANKS = 8 - TURN_BANKS
OUT_BUFS = 8

TILES = {
    "g_raw": ((BATCH, PACK, ROW), BF16, 1),
    "x_raw": ((4, BATCH, ROW), BF16, 1),
    "w1_raw0": ((4, BS), BF16, 1),
    "w1_raw1": ((4, BS), BF16, 1),
    "w2_raw0": ((4, BS), BF16, 1),
    "w2_raw1": ((4, BS), BF16, 1),
    "z_raw0": ((4, BS), F32, 1),
    "z_raw1": ((4, BS), F32, 1),
    "g_words": ((3, 4, P, PACK), BF16, 1),
    "w1_words": ((2, 4, P, PACK), BF16, 1),
    "w2_words": ((2, 4, P, PACK), BF16, 1),
    "x_words": ((3, 4, P, PACK), BF16, 1),
    "dz0": ((4, BS), BF16, 1),
    "dz1": ((4, BS), BF16, 1),
    "dzp_words": ((2, BS, PACK), BF16, 1),
    "dzk_words": ((2, 3, ROW, PACK), BF16, 1),
    "g_codes": ((3 * BS,), U32, 1),
    "g_scales": ((3 * BS,), U8, 1),
    "w1_codes": ((2 * BS,), U32, 2),
    "w1_scales": ((2 * BS,), U8, 2),
    "w2_codes": ((2 * BS,), U32, 1),
    "w2_scales": ((2 * BS,), U8, 1),
    "x_codes": ((3 * BS,), U32, 2),
    "x_scales": ((3 * BS,), U8, 2),
    "dzp_codes": ((2 * BS,), U32, 2),
    "dzp_scales": ((2 * BS,), U8, 2),
    "dzk_codes": ((6 * ROW,), U32, 2),
    "dzk_scales": ((6 * ROW,), U8, 2),
}

ORDER = """
load.w2/0 load.g/0*2 busy/0+3 load.w2/0 w2.turn/0+1 w2.turn/0+2 load.g/0*2 g.pack/0/v*2 load.w1/0*2 w2.pack/0/v
w2.pack/0/s w2.turn/0+2 w2.turn/0+3 w2.quant/0 g.pack/0/s load.z/0 g.pack/0/v w2.pack/0/s*2 g.quant/0
w1.turn/0*3 w1.pack/0/s*3 w2.quant/0 load.g/1*2 g.negate/0 dh0.mul/0 load.w2/1 g.quant-/0 w1.turn/0 dz0.mask/0
load.z/0 dh0.mul/0*3 w1.pack/0/s g.pack/1/s dz0.mask/0*3 dh1.mul/0 load.x/0*2 g.pack/1/s dzk0.turn/0*2
w1.quant/0 dh1.mul/0*2 load.w2/1 dzk0.pack/0/s dzp0.pack/0/v dzp0.pack/0/s w2.turn/1*2 dz1.mask/0*3 load.x/0*2
dzk0.pack/0/s dh1.mul/0 w2.pack/1/s*2 dzk1.turn/0+1 load.g/1*2 dz1.mask/0 dzp.quant/0 dzk1.pack/0/s dzk1.turn/0
w2.turn/1 w2.turn/1+2 load.z/1 dzk.negate/0 dzk1.pack/0/s dzp1.pack/0/v w2.pack/1/s*2 dzk.quant/0*2 x.turn/0*3
load.w1/1*2 x.pack/0/s*2 g.pack/1/v*2 dx0.mul/0*3 w2.quant/1 dx0.copy/0/s*2 dx1.mul/0 dx0.mul/0 g.quant/1
dx1.copy/0/s x.turn/0 dx0.copy/0/s*2 w1.turn/1 load.x/1 dzp1.pack/0/v dh0.mul/1*3 x.pack/0/s*2 load.z/1
g.negate/1 dzp.quant/0 dz0.mask/1*2 dx1.mul/0 dh0.mul/1 dx1.copy/0/s load.x/1*2 dx1.mul/0 g.quant-/1 w1.pack/1/s
w1.turn/1*2 dz0.mask/1*2 w1.pack/1/s*2 load.x/1 dh1.mul/1*3 x.quant/0 dx0.store/0 dx1.copy/0/s x.negate/0
w1.turn/1 dzp0.pack/1/v dzk0.turn/1*2 w1.pack/1/s dz1.mask/1*3 dx1.mul/0 dzk0.pack/1/s*2 dw0.mul/0*2
dx1.copy/0/s x.quant-/0 dh1.mul/1 dw0.copy/0/s*2 w1.quant/1 dw1.mul/0*3 dw1.copy/0/s*3 dz1.mask/1 dw0.store/0
dzp0.pack/1/v dzk1.turn/1*2 dx1.store/0 dzk.negate/1 x.turn/1 dzk1.pack/1/s*2 dzp1.pack/1/v dw0.mul/0*2
x.pack/1/v dw0.copy/0/s*2 dw1.mul/0 dw1.store/0 dzk.quant/1*2 x.turn/1*2 dw1.copy/0/s x.pack/1/s*2 dw0.store/0
dx0.mul/1*2 dzp1.pack/1/v dw1.store/0 dx1.mul/1*2 dx0.copy/1/v*2 x.turn/1 dzp.quant/1 dx0.store/1 dx1.copy/1/v
dx1.copy/1/s dx1.mul/1*2 x.pack/1/s dzp.quant/1 dx1.store/1 dx0.mul/1*2 dx1.copy/1/v dx1.copy/1/s x.quant/1
dx0.copy/1/s*2 dx1.store/1 x.negate/1 dw0.mul/1*3 dx0.store/1 x.quant-/1 dw0.copy/1/s dw0.copy/1/v dw0.store/1*2
dw1.mul/1*3 dw0.copy/1/s dw1.copy/1/v*3 dw0.store/1 dw1.mul/1 dw1.store/1*3 dw0.mul/1 dw1.copy/1/v dw0.copy/1/s
dw1.store/1 dw0.store/1
"""


def tile_scatteringmodule_pa_v_kernel(tc, xh, w1, w2, b1, b2, z1, grad_out, out_0, out_1):
    nc = tc.nc
    g_hbm = grad_out.rearrange("b (n p t) o h w r -> n b p (t o h w r)", n=NB, t=PACK)
    x_hbm = xh.rearrange("b (n p a) o h w r -> n b p a (o h w r)", n=NB, a=4)
    w_hbm = {
        "w1": w1.rearrange("r n (p a) k -> n r p a k", a=4),
        "w2": w2.rearrange("r n (p a) k -> n r p a k", a=4),
    }
    z_hbm = z1.rearrange("r n (p t) k -> n r p t k", t=4)
    dx_hbm = out_0.rearrange("b (n p a) o h w r -> n p b (a o h w r)", n=NB, a=4)
    dw_hbm = out_1.rearrange("r n (p a) k -> n r p a k", a=4)

    with ExitStack() as ctx:
        const = ctx.enter_context(tc.tile_pool(name="const", bufs=1))
        sbuf = ctx.enter_context(tc.tile_pool(name="sbuf", bufs=1))
        outs = ctx.enter_context(tc.tile_pool(name="outs", bufs=OUT_BUFS))
        turn_psum = ctx.enter_context(tc.psum_pool(name="turn_psum", bufs=TURN_BANKS))
        mul_psum = ctx.enter_context(tc.psum_pool(name="mul_psum", bufs=MUL_BANKS))

        ident = const.tile([P, P], F32, name="ident")
        make_identity(nc, ident[:])
        zeros = const.tile([P, BS], BF16, name="zeros")
        nc.gpsimd.memset(zeros[:], 0.0)

        made = {}
        banks = {}

        def sb(n, name):
            if (n, name) not in made:
                shape, dtype, bufs = TILES[name]
                made[n, name] = sbuf.tile([P] + list(shape), dtype, name=name, tag=name, bufs=bufs, align_bytes=64)
            return made[n, name]

        def out_tile(n, key, shape, bufs):
            if (n, key) not in made:
                tag = "out%d" % bufs
                made[n, key] = outs.tile(shape, F32, name=tag, tag=tag, bufs=bufs)
            return made[n, key]

        def move(engine):
            return {"v": nc.vector.tensor_copy, "s": nc.scalar.copy}[engine]

        def keep_busy(bank, count):
            for i in range(count):
                nc.tensor.matmul(bank, lhsT=zeros[:, 0:P], rhs=zeros[:], start=True, stop=True)

        def quantise(n, name, words, lo, hi, fmt):
            nc.vector.quantize_mx(
                out=sb(n, name + "_codes")[:, lo:hi].bitcast(fmt),
                scales=sb(n, name + "_scales")[:, lo:hi],
                in_=words[:, PACK * lo : PACK * hi],
            )

        def multiply(n, bank, left, left_fmt, right, right_fmt, columns):
            for i, (lo, ro) in enumerate(columns):
                nc.tensor.matmul_mx(
                    out=bank,
                    lhsT=sb(n, left + "_codes")[:, lo : lo + P].bitcast(left_fmt),
                    lhsT_scale=sb(n, left + "_scales")[:, lo : lo + P],
                    rhs=sb(n, right + "_codes")[:, ro : ro + BS].bitcast(right_fmt),
                    rhs_scale=sb(n, right + "_scales")[:, ro : ro + BS],
                    start=(i == 0),
                    stop=(i == len(columns) - 1),
                )

        def load_g(n, i, engine, idle):
            nc.sync.dma_start(out=sb(n, "g_raw")[:, i].rearrange("p t q -> p (t q)"), in_=g_hbm[n][i])

        def load_x(n, i, engine, idle):
            nc.sync.dma_start(out=sb(n, "x_raw")[:, :, i, :], in_=x_hbm[n][i])

        def load_w(which):
            def step(n, i, engine, idle):
                nc.sync.dma_start(out=sb(n, "%s_raw%d" % (which, i))[:], in_=w_hbm[which][n][i])

            return step

        def load_z(n, i, engine, idle):
            nc.sync.dma_start(out=sb(n, "z_raw%d" % i)[:], in_=z_hbm[n][i])

        def g_pack(n, i, engine, idle):
            src = sb(n, "g_raw")[:, i].rearrange("p t (m j r) -> p r m j t", j=4, r=2)
            dst = sb(n, "g_words")[:, RE : IM + 1, :, 32 * i : 32 * i + 32, :]
            move(engine)(out=dst.rearrange("p r j m t -> p r m j t"), in_=src)

        def g_words(n):
            return sb(n, "g_words")[:].rearrange("p s j m t -> p (s j m t)")

        def g_quant(n, i, engine, idle):
            quantise(n, "g", g_words(n), 0, BS * NEG, E5M2)

        def g_negate(n, i, engine, idle):
            g = sb(n, "g_words")[:].rearrange("p s j m t -> p s (j m t)")
            nc.vector.tensor_scalar_mul(out=g[:, NEG], in0=g[:, RE], scalar1=-1.0)

        def g_quant_negative(n, i, engine, idle):
            quantise(n, "g", g_words(n), BS * NEG, BS * (NEG + 1), E5M2)

        def w_turn(which):
            def step(n, i, engine, idle):
                part, half = divmod(i, 2)
                words = sb(n, "%s_raw%d" % (which, part))[:].rearrange("p a k -> p (a k)").bitcast(F32)
                bank = turn_psum.tile([P, 2, 2, P], F32, name="turn", tag="turn")
                keep_busy(bank[:].rearrange("p a u m -> p (a u m)"), idle)
                for a in range(2):
                    for u in range(2):
                        lo = ROW * (2 * half + a) + u
                        nc.tensor.transpose(bank[:, a, u, :], words[:, lo : lo + ROW - 1 : 2], ident[:])
                banks[n, which, i] = bank

            return step

        def w_pack(which):
            def step(n, i, engine, idle):
                part, half = divmod(i, 2)
                dst = sb(n, which + "_words")[:, part, 2 * half : 2 * half + 2]
                dst = dst.rearrange("p a m t -> p (a m t)").bitcast(F32)
                move(engine)(
                    out=dst.rearrange("p (a m u) -> p a m u", a=2, u=2),
                    in_=banks[n, which, i][:].rearrange("p a u m -> p a m u"),
                )

            return step

        def w_quant(which):
            def step(n, i, engine, idle):
                words = sb(n, which + "_words")[:].rearrange("p r a m t -> p (r a m t)")
                parts = (i,) if which == "w2" and n == 0 else (RE, IM)
                quantise(n, which, words, BS * parts[0], BS * (parts[-1] + 1), E4M3)

            return step

        def dh_mul(part):
            terms = ((RE, RE), (IM, IM)) if part == RE else ((IM, RE), (NEG, IM))

            def step(n, i, engine, idle):
                bank = mul_psum.tile([P, BS], F32, name="mul", tag="mul")
                columns = [(BS * g + P * i, BS * w) for g, w in terms]
                multiply(n, bank[:], "g", E5M2, "w2", E4M3, columns)
                banks[n, "dh%d" % part, i] = bank

            return step

        def dz_mask(part):
            def step(n, i, engine, idle):
                z = sb(n, "z_raw%d" % part)[:, i].rearrange("p (c u e) -> p u c e", u=2, e=2)
                dh = banks[n, "dh%d" % part, i][:].rearrange("p (u e c) -> p u c e", u=2, e=2)
                dz = sb(n, "dz%d" % part)[:, i].rearrange("p (u c e) -> p u c e", u=2, e=2)
                for u in range(2):
                    nc.vector.scalar_tensor_tensor(
                        out=dz[:, u], in0=z[:, u], scalar=0.0, in1=dh[:, u], op0=ALU.is_gt, op1=ALU.mult
                    )

            return step

        def dzp_pack(part):
            def step(n, i, engine, idle):
                k = slice(ROW * i, ROW * (i + 1))
                src = sb(n, "dz%d" % part)[:, :, k].rearrange("p t k -> p k t")
                move(engine)(out=sb(n, "dzp_words")[:, part, k, :], in_=src)

            return step

        def dzp_quant(n, i, engine, idle):
            words = sb(n, "dzp_words")[:].rearrange("p r k t -> p (r k t)")
            quantise(n, "dzp", words, BS * i, BS * (i + 1), E5M2)

        def dzk_turn(part):
            def step(n, i, engine, idle):
                words = sb(n, "dz%d" % part)[:].rearrange("p t k -> p (t k)").bitcast(F32)
                bank = turn_psum.tile([P, 2, 2, P], F32, name="turn", tag="turn")
                keep_busy(bank[:].rearrange("p e u m -> p (e u m)"), idle)
                for e in range(2):
                    for u in range(2):
                        lo = ROW * (2 * i + e) + P * u
                        nc.tensor.transpose(bank[:, e, u, :], words[:, lo : lo + P], ident[:])
                banks[n, "dzk%d" % part, i] = bank

            return step

        def dzk_pack(part):
            def step(n, i, engine, idle):
                dst = sb(n, "dzk_words")[:].rearrange("p h s q t -> p (h s q t)").bitcast(F32)
                dst = dst.rearrange("p (h s m x) -> p s h m x", h=2, s=3, x=8)[:, part]
                dst = dst[:, :, :, 4 * i : 4 * i + 4].rearrange("p h m (e u) -> p h m e u", e=2)
                src = banks[n, "dzk%d" % part, i][:].rearrange("p e u (h m) -> p h m e u", h=2)
                move(engine)(out=dst, in_=src)

            return step

        def dzk_negate(n, i, engine, idle):
            d = sb(n, "dzk_words")[:].rearrange("p h s q t -> p s h (q t)")
            nc.vector.tensor_scalar_mul(out=d[:, NEG], in0=d[:, RE], scalar1=-1.0)

        def dzk_quant(n, i, engine, idle):
            words = sb(n, "dzk_words")[:].rearrange("p h s q t -> p (h s q t)")
            lo, hi = ((0, 4 * ROW), (4 * ROW, 6 * ROW))[i]
            quantise(n, "dzk", words, lo, hi, E5M2)

        def x_turn(n, i, engine, idle):
            words = sb(n, "x_raw")[:].rearrange("p a b q -> p (a b q)").bitcast(F32)
            bank = turn_psum.tile([P, 4, P], F32, name="turn", tag="turn")
            keep_busy(bank[:].rearrange("p t m -> p (t m)"), idle)
            for t in range(4):
                lo = BS * i
                nc.tensor.transpose(bank[:, t, :], words[:, lo + t : lo + BS : 4], ident[:])
            banks[n, "x", i] = bank

        def x_pack(n, i, engine, idle):
            src = banks[n, "x", i][:].rearrange("p t m -> p (t m)").bitcast(BF16)
            move(engine)(
                out=sb(n, "x_words")[:, RE : IM + 1, i], in_=src.rearrange("p (t m r) -> p r m t", t=4, r=2)
            )

        def x_words(n):
            return sb(n, "x_words")[:].rearrange("p s a m t -> p (s a m t)")

        def x_quant(n, i, engine, idle):
            quantise(n, "x", x_words(n), 0, BS * NEG, E4M3)

        def x_negate(n, i, engine, idle):
            x = sb(n, "x_words")[:].rearrange("p s a m t -> p s (a m t)")
            nc.vector.tensor_scalar_mul(out=x[:, NEG], in0=x[:, IM], scalar1=-1.0)

        def x_quant_negative(n, i, engine, idle):
            quantise(n, "x", x_words(n), BS * NEG, BS * (NEG + 1), E4M3)

        def dw_mul(part):
            terms = ((RE, RE), (IM, IM)) if part == RE else ((RE, IM), (NEG, RE))

            def step(n, i, engine, idle):
                bank = mul_psum.tile([P, BS], F32, name="mul", tag="mul")
                columns = [(BS * x + P * i, BS * d) for x, d in terms]
                multiply(n, bank[:], "x", E4M3, "dzp", E5M2, columns)
                banks[n, "dw%d" % part, i] = bank

            return step

        def dw_copy(part):
            def step(n, i, engine, idle):
                out = out_tile(n, "dw%d_%d" % (part, i // 2), [P, 2, BS], OUT_BUFS)
                move(engine)(
                    out=out[:, i % 2].rearrange("p (c u e) -> p c u e", u=2, e=2),
                    in_=banks[n, "dw%d" % part, i][:].rearrange("p (u c e) -> p c u e", u=2, e=2),
                )

            return step

        def dw_store(part):
            def step(n, i, engine, idle):
                wide = 2 - n
                a = wide * i
                out = made[n, "dw%d_%d" % (part, a // 2)]
                nc.sync.dma_start(out=dw_hbm[n][part][:, a : a + wide], in_=out[:, a % 2 : a % 2 + wide])

            return step

        def dx_mul(half):
            def step(n, i, engine, idle):
                bank = mul_psum.tile([P, BS], F32, name="mul", tag="mul")
                lo = 3 * ROW * half
                columns = [(P * i, lo), (BS + P * i, lo + ROW)]
                multiply(n, bank[:], "w1", E4M3, "dzk", E5M2, columns)
                banks[n, "dx%d" % half, i] = bank

            return step

        def dx_wide(n):
            return 4 - 2 * n

        def dx_copy(half):
            def step(n, i, engine, idle):
                wide = dx_wide(n)
                bufs = 2 if n == 0 else OUT_BUFS
                out = out_tile(n, "dx%d_%d" % (half, i // wide), [P, 2, wide, ROW], bufs)
                move(engine)(
                    out=out[:, :, i % wide].rearrange("p b (q r) -> p b q r", r=2),
                    in_=banks[n, "dx%d" % half, i][:].rearrange("p (r b q) -> p b q r", r=2, b=2),
                )

            return step

        def dx_store(half):
            def step(n, i, engine, idle):
                wide = dx_wide(n)
                a = wide * i
                nc.sync.dma_start(
                    out=dx_hbm[n][:, 2 * half : 2 * half + 2, ROW * a : ROW * (a + wide)],
                    in_=made[n, "dx%d_%d" % (half, i)][:].rearrange("p b a q -> p b (a q)"),
                )

            return step

        def busy(n, i, engine, idle):
            bank = mul_psum.tile([P, BS], F32, name="mul", tag="mul")
            keep_busy(bank[:], idle)

        steps = {
            "load.g": load_g,
            "load.x": load_x,
            "load.z": load_z,
            "g.pack": g_pack,
            "g.quant": g_quant,
            "g.negate": g_negate,
            "g.quant-": g_quant_negative,
            "dzp.quant": dzp_quant,
            "dzk.negate": dzk_negate,
            "dzk.quant": dzk_quant,
            "x.turn": x_turn,
            "x.pack": x_pack,
            "x.quant": x_quant,
            "x.negate": x_negate,
            "x.quant-": x_quant_negative,
            "busy": busy,
        }
        for which in ("w1", "w2"):
            steps["load." + which] = load_w(which)
            steps[which + ".turn"] = w_turn(which)
            steps[which + ".pack"] = w_pack(which)
            steps[which + ".quant"] = w_quant(which)
        for part in (RE, IM):
            steps["dh%d.mul" % part] = dh_mul(part)
            steps["dz%d.mask" % part] = dz_mask(part)
            steps["dzp%d.pack" % part] = dzp_pack(part)
            steps["dzk%d.turn" % part] = dzk_turn(part)
            steps["dzk%d.pack" % part] = dzk_pack(part)
            steps["dw%d.mul" % part] = dw_mul(part)
            steps["dw%d.copy" % part] = dw_copy(part)
            steps["dw%d.store" % part] = dw_store(part)
        for half in range(2):
            steps["dx%d.mul" % half] = dx_mul(half)
            steps["dx%d.copy" % half] = dx_copy(half)
            steps["dx%d.store" % half] = dx_store(half)

        ctx.enter_context(tc.manual_schedule())
        taken = {}
        for token in ORDER.split():
            token, idle = token.split("+") if "+" in token else (token, "0")
            token, count = token.split("*") if "*" in token else (token, "1")
            kind, block, engine = (token + "/").split("/")[0:3]
            n = int(block)
            for repeat in range(int(count)):
                i = taken.setdefault((kind, n), 0)
                taken[kind, n] = i + 1
                steps[kind](n, i, engine, int(idle))
